import numpy as np
import ml_dtypes


def mxq(x, axis, fmt="e4m3"):
    dtype, down = {"e4m3": (ml_dtypes.float8_e4m3fn, 7), "e5m2": (ml_dtypes.float8_e5m2, 14)}[fmt]
    v = np.moveaxis(np.asarray(x, np.float32).astype(ml_dtypes.bfloat16).astype(np.float64), axis, -1)
    blocks = v.reshape(v.shape[:-1] + (-1, 32))
    amax = np.abs(blocks).max(-1, keepdims=True)
    byte = np.maximum(np.where(amax > 0, np.frexp(amax)[1] - 1 + 127, 0) - down, 1)
    scale = np.exp2(byte - 127.0)
    codes = (blocks / scale).astype(np.float32).astype(dtype).astype(np.float64)
    return np.moveaxis((codes * scale).reshape(v.shape), -1, axis)


WIDE = False


def mx_kscale(k):
    if not WIDE:
        return np.ones(k)
    levels = np.array([30, -30])
    if k % 512:
        return np.exp2(np.random.permutation(np.resize(levels, k // 32))).repeat(32)
    a = np.empty((k // 512, 16))
    for p in range(k // 512):
        a[p, :8] = np.random.permutation(np.resize(levels, 8))
        for g in range(8):
            far = levels[np.abs(levels - a[p, g]) >= 10]
            a[p, g + 8] = far[np.random.randint(len(far))]
    return np.exp2(a.ravel()).repeat(32)


BF16 = ml_dtypes.bfloat16


def bf(x):
    return np.asarray(x, np.float32).astype(BF16)


def f64(x):
    return np.asarray(x).astype(np.float64)


B, S, M, U, V, H, W = 1, 1024, 1536, 12, 4, 128, 512
WAVELENGTH = 10000.0
ROPE_SCALE = 1.0


def rope(x):
    inv_freq = 1.0 / (WAVELENGTH ** (np.arange(0, H, 2).astype(np.float64) / H))
    pos = np.arange(S).astype(np.float64) / ROPE_SCALE
    f = pos[:, None] * inv_freq[None, :]
    emb = np.concatenate([f, f], axis=-1)
    cos = np.cos(emb)[None, :, None, :]
    sin = np.sin(emb)[None, :, None, :]
    x1, x2 = np.split(x, 2, axis=-1)
    rot = np.concatenate([-x2, x1], axis=-1)
    return x * cos + rot * sin


def setup_inputs():
    s = mx_kscale(M)
    c = 1.0 / np.sqrt(M)
    return {"hidden_states": bf(np.random.standard_normal((B, S, M)) * s),
            "Wq": bf(np.random.standard_normal((M, U, H)) * c / s[:, None, None]),
            "bq": bf(np.random.standard_normal((U, H)) * 0.3),
            "Wk": bf(np.random.standard_normal((M, V, H)) * c / s[:, None, None]),
            "bk": bf(np.random.standard_normal((V, H)) * 0.3),
            "Wv": bf(np.random.standard_normal((M, V, H)) * 2.0 * c / s[:, None, None]),
            "bv": bf(np.random.standard_normal((V, H)) * 0.3)}


def reference(hidden_states, Wq, bq, Wk, bk, Wv, bv):
    xq = mxq(f64(hidden_states), 2, "e5m2")
    q = (xq @ mxq(f64(Wq).reshape(M, U * H), 0, "e5m2")).reshape(B, S, U, H) + f64(bq)
    k = (xq @ mxq(f64(Wk).reshape(M, V * H), 0, "e5m2")).reshape(B, S, V, H) + f64(bk)
    v = (xq @ mxq(f64(Wv).reshape(M, V * H), 0, "e5m2")).reshape(B, S, V, H) + f64(bv)
    return rope(q), rope(k), v

@@ -1,0 +1,383 @@
+from contextlib import ExitStack
+
+import concourse.mybir as mybir
+from concourse.masks import make_identity
+
+FLOPS = 2 * 1024 * 1536 * 2560
+
+F32 = mybir.dt.float32
+BF16 = mybir.dt.bfloat16
+I32 = mybir.dt.int32
+U32 = mybir.dt.uint32
+U8 = mybir.dt.uint8
+E5X4 = mybir.dt.float8_e5m2_x4
+ALU = mybir.AluOpType
+ACT = mybir.ActivationFunctionType
+
+P = 128
+PI = 3.141592653589793
+KP = 512
+PASSES = 3
+HALF = 512
+TABW = 514
+LAG = 2
+
+QUADS = [(0, 0), (1, 0), (0, 1), (1, 1), (2, 0), (2, 1), (3, 0), (3, 1)]
+
+WI_PLAN = {
+    (0, 0): [("g", 0, 512)],
+    (0, 1): [("s", 0, 256), ("g", 256, 512)],
+    (0, 2): [("g", 0, 192), ("s", 192, 352), ("v", 352, 512)],
+    (1, 0): [("g", 0, 512)],
+    (1, 1): [("s", 0, 512)],
+    (1, 2): [("g", 0, 512)],
+}
+WI_DEFAULT = [[("s", 0, 256), ("s", 256, 512)], [("s", 0, 256), ("s", 256, 512)], [("g", 0, 256), ("g", 256, 512)]]
+
+WI_STEP = {
+    (2, 0): 2, (2, 1): 3, (2, 2): 4,
+    (3, 0): 6, (3, 1): 7, (3, 2): 8,
+    (4, 0): 10, (4, 1): 11, (4, 2): 12,
+}
+
+
+def tile_qwenattention_pa_kernel(tc, hidden_states, Wq, bq, Wk, bk, Wv, bv, out_0, out_1, out_2):
+    nc = tc.nc
+    x2 = hidden_states.rearrange("o s m -> (o s) m")
+    w2 = [Wq.rearrange("m u h -> m (u h)"), Wk.rearrange("m u h -> m (u h)"), Wv.rearrange("m u h -> m (u h)")]
+    o2 = [
+        out_0.rearrange("o s u h -> (o s) (u h)"),
+        out_1.rearrange("o s u h -> (o s) (u h)"),
+        out_2.rearrange("o s u h -> (o s) (u h)"),
+    ]
+
+    def w_src(g, c):
+        rows = slice(c * KP, (c + 1) * KP)
+        if g < 3:
+            return w2[0][rows, g * 512 : (g + 1) * 512]
+        return w2[g - 2][rows, :]
+
+    def o_dst(g, t):
+        rows = slice(t * HALF, (t + 1) * HALF)
+        if g < 3:
+            return o2[0][rows, g * 512 : (g + 1) * 512]
+        return o2[g - 2][rows, :]
+
+    with ExitStack() as ctx:
+        const = ctx.enter_context(tc.tile_pool(name="const", bufs=1))
+        work = ctx.enter_context(tc.tile_pool(name="work", bufs=2))
+        psum = ctx.enter_context(tc.psum_pool(name="psum", bufs=4))
+        ctx.enter_context(tc.manual_schedule())
+
+        xraw = {}
+        wraw = {}
+        xbank = {}
+        xg = {}
+        wg = {}
+        xq = {}
+        xs = {}
+        wq = {}
+        ws = {}
+        acc = {}
+        ut = {}
+        wt = {}
+        ybank = {}
+        ystage = {}
+
+        def load_x(t, c):
+            xraw[(t, c)] = const.tile([P, 4, KP], BF16, name="xraw%d%d" % (t, c))
+            src = x2[t * HALF : (t + 1) * HALF, c * KP : (c + 1) * KP]
+            nc.sync.dma_start(out=xraw[(t, c)][:], in_=src.rearrange("(b p) k -> p b k", p=P))
+
+        def load_w(g, c):
+            wraw[(g, c)] = work.tile([P, 4, 512], BF16, name="wraw", tag="wraw", bufs=8)
+            nc.sync.dma_start(out=wraw[(g, c)][:], in_=w_src(g, c).rearrange("(p j) n -> p j n", j=4))
+
+        def x_transpose(t, c):
+            words = xraw[(t, c)][:].rearrange("p b k -> p (b k)").bitcast(F32)
+            for half in range(2):
+                bank = psum.tile([P, 2, 2, P], F32, name="xt", tag="tp", bufs=4)
+                xbank[(t, c, half)] = bank
+                for b2 in range(2):
+                    b = 2 * half + b2
+                    for u in range(2):
+                        nc.tensor.transpose(bank[:, b2, u, :], words[:, b * 256 + u : (b + 1) * 256 : 2], ident[:])
+
+        def x_evac(t, c, engines):
+            xg[(t, c)] = work.tile([P, HALF, 4], BF16, name="xg", tag="xg", bufs=3, align_bytes=64)
+            gw = xg[(t, c)][:].rearrange("p r t -> p (r t)").bitcast(F32)
+            for half in range(2):
+                dst = gw[:, half * 512 : (half + 1) * 512].rearrange("p (b r u) -> p b r u", b=2, u=2)
+                src = xbank[(t, c, half)][:].rearrange("p b u r -> p b r u")
+                if engines[half] == "v":
+                    nc.vector.tensor_copy(out=dst, in_=src)
+                else:
+                    nc.scalar.copy(out=dst, in_=src)
+
+        def x_quant(t, c):
+            xq[(t, c)] = const.tile([P, HALF], U32, name="xq%d%d" % (t, c), align_bytes=64)
+            xs[(t, c)] = const.tile([P, HALF], U8, name="xs%d%d" % (t, c), align_bytes=64)
+            nc.vector.quantize_mx(
+                out=xq[(t, c)][:].bitcast(E5X4), scales=xs[(t, c)][:], in_=xg[(t, c)][:].rearrange("p r t -> p (r t)")
+            )
+
+        def w_interleave(g, c):
+            wg[(g, c)] = work.tile([P, 512, 4], BF16, name="wg", tag="wg", bufs=4, align_bytes=64)
+            for eng, n0, n1 in WI_PLAN.get((g, c), WI_DEFAULT[c]):
+                dst = wg[(g, c)][:, n0:n1, :]
+                src = wraw[(g, c)][:, :, n0:n1].rearrange("p j n -> p n j")
+                if eng == "v":
+                    nc.vector.tensor_copy(out=dst, in_=src)
+                elif eng == "s":
+                    nc.scalar.copy(out=dst, in_=src)
+                else:
+                    nc.gpsimd.tensor_scalar(out=dst, in0=src, scalar1=1.0, scalar2=0.0, op0=ALU.mult, op1=ALU.add)
+
+        def w_quant(g, c):
+            wq[(g, c)] = const.tile([P, 512], U32, name="wq%d%d" % (g, c), align_bytes=64)
+            ws[(g, c)] = const.tile([P, 512], U8, name="ws%d%d" % (g, c), align_bytes=64)
+            nc.vector.quantize_mx(
+                out=wq[(g, c)][:].bitcast(E5X4), scales=ws[(g, c)][:], in_=wg[(g, c)][:].rearrange("p n j -> p (n j)")
+            )
+
+        def unit_of(n):
+            g, t = QUADS[n // 4]
+            return g, t, n % 4
+
+        def mx_pass(n, c):
+            g, t, h = unit_of(n)
+            if c == 0:
+                acc[n] = psum.tile([P, HALF], F32, name="acc", tag="mx", bufs=4)
+            cols = slice(h * P, (h + 1) * P)
+            nc.tensor.matmul_mx(
+                out=acc[n][:],
+                lhsT=wq[(g, c)][:, cols].bitcast(E5X4),
+                lhsT_scale=ws[(g, c)][:, cols],
+                rhs=xq[(t, c)][:].bitcast(E5X4),
+                rhs_scale=xs[(t, c)][:],
+                start=(c == 0),
+                stop=(c == PASSES - 1),
+            )
+
+        def rope_products(n):
+            g, t, h = unit_of(n)
+            hd = 4 * g + h
+            ut[n] = work.tile([P, HALF], F32, name="ut", tag="ut", bufs=6)
+            wt[n] = work.tile([P, HALF], F32, name="wt", tag="wt", bufs=6)
+            nc.vector.scalar_tensor_tensor(
+                out=ut[n][:], in0=acc[n][:], scalar=bcol[:, hd : hd + 1], in1=ctab[t][:, 0:HALF], op0=ALU.add, op1=ALU.mult
+            )
+            nc.vector.scalar_tensor_tensor(
+                out=wt[n][:], in0=acc[n][:], scalar=bcol[:, hd : hd + 1], in1=stab[t][:, 0:HALF], op0=ALU.add, op1=ALU.mult
+            )
+
+        def turn_and_add(n):
+            ybank[n] = psum.tile([P, 4, P], F32, name="yb", tag="tp", bufs=4)
+            for b in range(4):
+                cols = slice(b * P, (b + 1) * P)
+                nc.tensor.matmul(out=ybank[n][:, b, :], lhsT=ut[n][:, cols], rhs=ident[:], is_transpose=True, start=True, stop=False)
+                nc.tensor.matmul(out=ybank[n][:, b, :], lhsT=wt[n][:, cols], rhs=swap[:], is_transpose=True, start=False, stop=True)
+
+        def y_evac(n):
+            g, t, h = unit_of(n)
+            if h == 0:
+                ystage[(g, t)] = work.tile([P, 4, 512], F32, name="yst", tag="yst", bufs=3)
+            nc.scalar.copy(out=ystage[(g, t)][:, :, h * P : (h + 1) * P], in_=ybank[n][:])
+            if h == 3:
+                nc.sync.dma_start(out=o_dst(g, t).rearrange("(b p) n -> p b n", p=P), in_=ystage[(g, t)][:])
+
+        def v_pass(vb, c):
+            t, b = vb // 4, vb % 4
+            if c == 0:
+                acc[("v", vb)] = psum.tile([P, 512], F32, name="acc", tag="mx", bufs=4)
+            cols = slice(b * P, (b + 1) * P)
+            nc.tensor.matmul_mx(
+                out=acc[("v", vb)][:],
+                lhsT=xq[(t, c)][:, cols].bitcast(E5X4),
+                lhsT_scale=xs[(t, c)][:, cols],
+                rhs=wq[(4, c)][:].bitcast(E5X4),
+                rhs_scale=ws[(4, c)][:],
+                start=(c == 0),
+                stop=(c == PASSES - 1),
+            )
+
+        def v_finish(vb):
+            t, b = vb // 4, vb % 4
+            if b % 2 == 0:
+                ystage[("v", vb // 2)] = work.tile([P, 2, 512], F32, name="vst", tag="vst", bufs=4)
+            st = ystage[("v", vb // 2)]
+            nc.vector.tensor_tensor(out=st[:, b % 2, :], in0=acc[("v", vb)][:], in1=bvb[:], op=ALU.add)
+            if b % 2 == 1:
+                rows = slice((vb - 1) * P, (vb + 1) * P)
+                nc.sync.dma_start(out=o2[2][rows, :].rearrange("(b p) n -> p b n", p=P), in_=st[:])
+
+        browb = const.tile([P, P], BF16, name="browb")
+        nc.vector.memset(browb[:], 0.0)
+        bvrow = const.tile([P, 512], BF16, name="bvrow")
+        nc.vector.memset(bvrow[:], 0.0)
+        nc.scalar.dma_start(out=browb[0:12, :], in_=bq)
+        nc.scalar.dma_start(out=browb[12:16, :], in_=bk)
+        nc.scalar.dma_start(out=browb[16:20, :], in_=bv)
+        nc.scalar.dma_start(out=bvrow[0:1, :], in_=bv.rearrange("(o v) h -> o (v h)", o=1))
+        for c in range(PASSES):
+            load_x(0, c)
+            load_w(0, c)
+        for c in range(PASSES):
+            load_w(1, c)
+        for c in range(PASSES):
+            load_x(1, c)
+        load_w(2, 0)
+        load_w(2, 1)
+        late_loads = [(2, 2), (3, 0), (3, 1), (3, 2), (4, 0), (4, 1), (4, 2)]
+
+        ident = const.tile([P, P], F32, name="ident")
+        make_identity(nc, ident[:])
+        tokf = const.tile([P, TABW], F32, name="tokf")
+        nc.gpsimd.iota(tokf[:], pattern=[[1, TABW]], base=0, channel_multiplier=0, allow_small_or_imprecise_dtypes=True)
+
+        one = const.tile([P, 1], F32, name="one")
+        nc.vector.memset(one[:], 1.0)
+        junk = const.tile([P, 1], F32, name="junk")
+        nc.scalar.activation(out=junk[:], in_=one[:], func=ACT.Sin)
+
+
+        grow = const.tile([P, P], F32, name="grow")
+        nc.vector.tensor_scalar(out=grow[:, 0:1], in0=one[:], scalar1=1.0 / (2.0 * PI), scalar2=None, op0=ALU.mult)
+        onesb = const.tile([P, P], BF16, name="onesb")
+        phase = const.tile([P, 2], F32, name="phase")
+        sgn = const.tile([P, 2], F32, name="sgn")
+        for s in (1, 2, 4, 8, 16, 32):
+            nc.vector.tensor_scalar(
+                out=grow[:, s : 2 * s], in0=grow[:, 0:s], scalar1=10000.0 ** (-s / 64.0), scalar2=None, op0=ALU.mult
+            )
+        nc.vector.tensor_copy(out=grow[:, 64:128], in_=grow[:, 0:64])
+        gps = psum.tile([P, P], F32, name="gps", tag="tp", bufs=4)
+        nc.tensor.transpose(gps[:], grow[:], ident[:])
+        nc.vector.memset(onesb[:], 1.0)
+        nc.vector.memset(phase[:, 0:1], 0.25)
+        nc.vector.memset(phase[:, 1:2], 0.0)
+        nc.vector.tensor_scalar(out=sgn[:, 0:1], in0=one[:], scalar1=-2.0 * PI, scalar2=None, op0=ALU.mult)
+        nc.vector.tensor_scalar(out=sgn[0:64, 1:2], in0=one[0:64, :], scalar1=-2.0 * PI, scalar2=None, op0=ALU.mult)
+        nc.vector.tensor_scalar(out=sgn[64:128, 1:2], in0=one[64:128, :], scalar1=2.0 * PI, scalar2=None, op0=ALU.mult)
+        gcol = const.tile([P, 1], F32, name="gcol")
+        nc.vector.tensor_copy(out=gcol[:], in_=gps[:, 0:1])
+
+        turns = work.tile([P, 2, TABW], F32, name="turns", tag="yst", bufs=3)
+        whole = work.tile([P, 2, TABW], I32, name="whole", tag="yst", bufs=3)
+        for j in range(2):
+            nc.vector.tensor_scalar(
+                out=turns[:, j, :], in0=tokf[:], scalar1=gcol[:, 0:1], scalar2=phase[:, j : j + 1], op0=ALU.mult, op1=ALU.add
+            )
+        nc.vector.tensor_copy(out=whole[:], in_=turns[:])
+        nc.vector.tensor_tensor(out=turns[:], in0=turns[:], in1=whole[:], op=ALU.subtract)
+        nc.vector.scalar_tensor_tensor(out=turns[:], in0=turns[:], scalar=0.5, in1=turns[:], op0=ALU.is_gt, op1=ALU.subtract)
+        ctab = [const.tile([P, TABW], F32, name="ctab0"), const.tile([P, HALF], F32, name="ctab1")]
+        stab = [const.tile([P, TABW], F32, name="stab0"), const.tile([P, HALF], F32, name="stab1")]
+
+        x_transpose(0, 0)
+        x_evac(0, 0, "ss")
+        w_interleave(0, 0)
+        x_transpose(0, 1)
+        x_quant(0, 0)
+        x_evac(0, 1, "vs")
+        w_quant(0, 0)
+        for n in range(4):
+            mx_pass(n, 0)
+        w_interleave(0, 1)
+
+        brow = const.tile([P, P], F32, name="brow")
+        nc.vector.tensor_copy(out=brow[:], in_=browb[:])
+        swap = const.tile([P, P], F32, name="swap")
+        nc.vector.tensor_copy(out=swap[:, 0:64], in_=ident[:, 64:128])
+        nc.vector.tensor_copy(out=swap[:, 64:128], in_=ident[:, 0:64])
+        x_transpose(0, 2)
+        bps = psum.tile([P, P], F32, name="bps", tag="tp", bufs=4)
+        nc.tensor.transpose(bps[:], brow[:], ident[:])
+        x_quant(0, 1)
+        w_quant(0, 1)
+        for n in range(4):
+            mx_pass(n, 1)
+        x_evac(0, 2, "vs")
+        w_interleave(0, 2)
+        x_quant(0, 2)
+        w_quant(0, 2)
+        nc.scalar.activation(out=ctab[0][:], in_=turns[:, 0, :], func=ACT.Sin, scale=sgn[:, 0:1])
+        nc.scalar.activation(out=stab[0][:], in_=turns[:, 1, :], func=ACT.Sin, scale=sgn[:, 1:2])
+        bcol = const.tile([P, 20], F32, name="bcol")
+        nc.vector.tensor_copy(out=bcol[:], in_=bps[:, 0:20])
+        for n in range(4):
+            mx_pass(n, 2)
+
+        w_interleave(1, 0)
+        w_interleave(1, 1)
+        w_interleave(1, 2)
+
+        nsin = const.tile([P, 1], F32, name="nsin")
+        tmpc = const.tile([P, HALF], F32, name="tmpc")
+        tmps = const.tile([P, HALF], F32, name="tmps")
+        nc.gpsimd.tensor_scalar(out=tmpc[:], in0=ctab[0][:, 0:HALF], scalar1=ctab[0][:, 512:513], scalar2=0.0, op0=ALU.mult, op1=ALU.add)
+        nc.gpsimd.tensor_scalar(out=tmps[:], in0=stab[0][:, 0:HALF], scalar1=ctab[0][:, 512:513], scalar2=0.0, op0=ALU.mult, op1=ALU.add)
+
+        bvps = psum.tile([P, 512], F32, name="bvps", tag="tp", bufs=4)
+        nc.tensor.matmul(out=bvps[:], lhsT=onesb[:], rhs=bvrow[:], start=True, stop=True)
+        bvb = const.tile([P, 512], F32, name="bvb")
+        nc.scalar.copy(out=bvb[:], in_=bvps[:])
+
+        rope_products(0)
+        w_quant(1, 0)
+        rope_products(1)
+        w_quant(1, 1)
+        x_transpose(1, 0)
+        x_evac(1, 0, "ss")
+        rope_products(2)
+        w_quant(1, 2)
+        rope_products(3)
+        nc.vector.tensor_scalar(out=nsin[:], in0=stab[0][:, 512:513], scalar1=-1.0, scalar2=None, op0=ALU.mult)
+        nc.vector.scalar_tensor_tensor(
+            out=ctab[1][:], in0=stab[0][:, 0:HALF], scalar=nsin[:, 0:1], in1=tmpc[:], op0=ALU.mult, op1=ALU.add
+        )
+        nc.vector.scalar_tensor_tensor(
+            out=stab[1][:], in0=ctab[0][:, 0:HALF], scalar=stab[0][:, 512:513], in1=tmps[:], op0=ALU.mult, op1=ALU.add
+        )
+
+        for k in range(2, 16 + 4 + LAG):
+            if k == 2:
+                x_quant(1, 0)
+                x_transpose(1, 1)
+                x_evac(1, 1, "ss")
+            if k == 3:
+                x_quant(1, 1)
+                x_transpose(1, 2)
+                x_evac(1, 2, "ss")
+            for gc in sorted(WI_STEP):
+                if WI_STEP[gc] == k:
+                    w_interleave(gc[0], gc[1])
+                    if late_loads:
+                        nxt = late_loads[0]
+                        late_loads.remove(nxt)
+                        load_w(nxt[0], nxt[1])
+            if k in (2, 3, 4) and late_loads:
+                nxt = late_loads[0]
+                late_loads.remove(nxt)
+                load_w(nxt[0], nxt[1])
+            if k < 16:
+                for n in (2 * k, 2 * k + 1):
+                    for c in range(PASSES):
+                        mx_pass(n, c)
+                rope_products(2 * k)
+                if k == 3:
+                    x_quant(1, 2)
+                for gc in sorted(WI_STEP):
+                    if WI_STEP[gc] + 1 == k:
+                        w_quant(gc[0], gc[1])
+                rope_products(2 * k + 1)
+            elif k < 20:
+                for vb in (2 * (k - 16), 2 * (k - 16) + 1):
+                    for c in range(PASSES):
+                        v_pass(vb, c)
+                    v_finish(vb)
+            j = k - LAG
+            if j < 16:
+                for n in (2 * j, 2 * j + 1):
+                    turn_and_add(n)
+                    y_evac(n)

@@ -20,24 +20,24 @@ KP = 512
 PASSES = 3
 HALF = 512
 TABW = 514
-LAG = 2
+MXB = 4
+TPB = 4
+LAG = 1
 
-QUADS = [(0, 0), (1, 0), (0, 1), (1, 1), (2, 0), (2, 1), (3, 0), (3, 1)]
+QUADS = [(0, 0), (0, 1), (1, 0), (1, 1), (2, 0), (2, 1), (3, 0), (3, 1)]
 
 WI_PLAN = {
-    (0, 0): [("g", 0, 512)],
-    (0, 1): [("s", 0, 256), ("g", 256, 512)],
-    (0, 2): [("g", 0, 192), ("s", 192, 352), ("v", 352, 512)],
-    (1, 0): [("g", 0, 512)],
-    (1, 1): [("s", 0, 512)],
-    (1, 2): [("g", 0, 512)],
+    (0, 0): [("v", 0, 512)],
+    (0, 1): [("s", 0, 512)],
+    (0, 2): [("s", 0, 192), ("v", 192, 512)],
 }
-WI_DEFAULT = [[("s", 0, 256), ("s", 256, 512)], [("s", 0, 256), ("s", 256, 512)], [("g", 0, 256), ("g", 256, 512)]]
+WI_DEFAULT = [[("s", 0, 256), ("s", 256, 512)], [("s", 0, 256), ("s", 256, 512)], [("s", 0, 256), ("s", 256, 512)]]
 
 WI_STEP = {
-    (2, 0): 2, (2, 1): 3, (2, 2): 4,
-    (3, 0): 6, (3, 1): 7, (3, 2): 8,
-    (4, 0): 10, (4, 1): 11, (4, 2): 12,
+    (1, 0): 1, (1, 1): 2, (1, 2): 2,
+    (2, 0): 4, (2, 1): 5, (2, 2): 6,
+    (3, 0): 8, (3, 1): 9, (3, 2): 10,
+    (4, 0): 12, (4, 1): 13, (4, 2): 14,
 }
 
 
@@ -96,7 +96,7 @@ def tile_qwenattention_pa_kernel(tc, hidden_states, Wq, bq, Wk, bk, Wv, bv, out_
         def x_transpose(t, c):
             words = xraw[(t, c)][:].rearrange("p b k -> p (b k)").bitcast(F32)
             for half in range(2):
-                bank = psum.tile([P, 2, 2, P], F32, name="xt", tag="tp", bufs=4)
+                bank = psum.tile([P, 2, 2, P], F32, name="xt", tag="tp", bufs=TPB)
                 xbank[(t, c, half)] = bank
                 for b2 in range(2):
                     b = 2 * half + b2
@@ -147,7 +147,7 @@ def tile_qwenattention_pa_kernel(tc, hidden_states, Wq, bq, Wk, bk, Wv, bv, out_
         def mx_pass(n, c):
             g, t, h = unit_of(n)
             if c == 0:
-                acc[n] = psum.tile([P, HALF], F32, name="acc", tag="mx", bufs=4)
+                acc[n] = psum.tile([P, HALF], F32, name="acc", tag="mx", bufs=MXB)
             cols = slice(h * P, (h + 1) * P)
             nc.tensor.matmul_mx(
                 out=acc[n][:],
@@ -172,7 +172,7 @@ def tile_qwenattention_pa_kernel(tc, hidden_states, Wq, bq, Wk, bk, Wv, bv, out_
             )
 
         def turn_and_add(n):
-            ybank[n] = psum.tile([P, 4, P], F32, name="yb", tag="tp", bufs=4)
+            ybank[n] = psum.tile([P, 4, P], F32, name="yb", tag="tp", bufs=TPB)
             for b in range(4):
                 cols = slice(b * P, (b + 1) * P)
                 nc.tensor.matmul(out=ybank[n][:, b, :], lhsT=ut[n][:, cols], rhs=ident[:], is_transpose=True, start=True, stop=False)
@@ -189,7 +189,7 @@ def tile_qwenattention_pa_kernel(tc, hidden_states, Wq, bq, Wk, bk, Wv, bv, out_
         def v_pass(vb, c):
             t, b = vb // 4, vb % 4
             if c == 0:
-                acc[("v", vb)] = psum.tile([P, 512], F32, name="acc", tag="mx", bufs=4)
+                acc[("v", vb)] = psum.tile([P, 512], F32, name="acc", tag="mx", bufs=MXB)
             cols = slice(b * P, (b + 1) * P)
             nc.tensor.matmul_mx(
                 out=acc[("v", vb)][:],
@@ -223,11 +223,9 @@ def tile_qwenattention_pa_kernel(tc, hidden_states, Wq, bq, Wk, bk, Wv, bv, out_
             load_x(0, c)
             load_w(0, c)
         for c in range(PASSES):
-            load_w(1, c)
-        for c in range(PASSES):
             load_x(1, c)
-        load_w(2, 0)
-        load_w(2, 1)
+        for g, c in [(1, 0), (1, 1), (1, 2), (2, 0), (2, 1)]:
+            load_w(g, c)
         late_loads = [(2, 2), (3, 0), (3, 1), (3, 2), (4, 0), (4, 1), (4, 2)]
 
         ident = const.tile([P, P], F32, name="ident")
@@ -240,7 +238,6 @@ def tile_qwenattention_pa_kernel(tc, hidden_states, Wq, bq, Wk, bk, Wv, bv, out_
         junk = const.tile([P, 1], F32, name="junk")
         nc.scalar.activation(out=junk[:], in_=one[:], func=ACT.Sin)
 
-
         grow = const.tile([P, P], F32, name="grow")
         nc.vector.tensor_scalar(out=grow[:, 0:1], in0=one[:], scalar1=1.0 / (2.0 * PI), scalar2=None, op0=ALU.mult)
         onesb = const.tile([P, P], BF16, name="onesb")
@@ -251,7 +248,7 @@ def tile_qwenattention_pa_kernel(tc, hidden_states, Wq, bq, Wk, bk, Wv, bv, out_
                 out=grow[:, s : 2 * s], in0=grow[:, 0:s], scalar1=10000.0 ** (-s / 64.0), scalar2=None, op0=ALU.mult
             )
         nc.vector.tensor_copy(out=grow[:, 64:128], in_=grow[:, 0:64])
-        gps = psum.tile([P, P], F32, name="gps", tag="tp", bufs=4)
+        gps = psum.tile([P, P], F32, name="gps", tag="tp", bufs=TPB)
         nc.tensor.transpose(gps[:], grow[:], ident[:])
         nc.vector.memset(onesb[:], 1.0)
         nc.vector.memset(phase[:, 0:1], 0.25)
@@ -268,87 +265,26 @@ def tile_qwenattention_pa_kernel(tc, hidden_states, Wq, bq, Wk, bk, Wv, bv, out_
             nc.vector.tensor_scalar(
                 out=turns[:, j, :], in0=tokf[:], scalar1=gcol[:, 0:1], scalar2=phase[:, j : j + 1], op0=ALU.mult, op1=ALU.add
             )
-        nc.vector.tensor_copy(out=whole[:], in_=turns[:])
-        nc.vector.tensor_tensor(out=turns[:], in0=turns[:], in1=whole[:], op=ALU.subtract)
-        nc.vector.scalar_tensor_tensor(out=turns[:], in0=turns[:], scalar=0.5, in1=turns[:], op0=ALU.is_gt, op1=ALU.subtract)
-        ctab = [const.tile([P, TABW], F32, name="ctab0"), const.tile([P, HALF], F32, name="ctab1")]
-        stab = [const.tile([P, TABW], F32, name="stab0"), const.tile([P, HALF], F32, name="stab1")]
-
-        x_transpose(0, 0)
-        x_evac(0, 0, "ss")
-        w_interleave(0, 0)
-        x_transpose(0, 1)
-        x_quant(0, 0)
-        x_evac(0, 1, "vs")
-        w_quant(0, 0)
-        for n in range(4):
-            mx_pass(n, 0)
-        w_interleave(0, 1)
-
         brow = const.tile([P, P], F32, name="brow")
         nc.vector.tensor_copy(out=brow[:], in_=browb[:])
-        swap = const.tile([P, P], F32, name="swap")
-        nc.vector.tensor_copy(out=swap[:, 0:64], in_=ident[:, 64:128])
-        nc.vector.tensor_copy(out=swap[:, 64:128], in_=ident[:, 0:64])
-        x_transpose(0, 2)
-        bps = psum.tile([P, P], F32, name="bps", tag="tp", bufs=4)
+        bps = psum.tile([P, P], F32, name="bps", tag="tp", bufs=TPB)
         nc.tensor.transpose(bps[:], brow[:], ident[:])
-        x_quant(0, 1)
-        w_quant(0, 1)
-        for n in range(4):
-            mx_pass(n, 1)
-        x_evac(0, 2, "vs")
-        w_interleave(0, 2)
-        x_quant(0, 2)
-        w_quant(0, 2)
-        nc.scalar.activation(out=ctab[0][:], in_=turns[:, 0, :], func=ACT.Sin, scale=sgn[:, 0:1])
-        nc.scalar.activation(out=stab[0][:], in_=turns[:, 1, :], func=ACT.Sin, scale=sgn[:, 1:2])
-        bcol = const.tile([P, 20], F32, name="bcol")
-        nc.vector.tensor_copy(out=bcol[:], in_=bps[:, 0:20])
-        for n in range(4):
-            mx_pass(n, 2)
-
-        w_interleave(1, 0)
-        w_interleave(1, 1)
-        w_interleave(1, 2)
-
-        nsin = const.tile([P, 1], F32, name="nsin")
-        tmpc = const.tile([P, HALF], F32, name="tmpc")
-        tmps = const.tile([P, HALF], F32, name="tmps")
-        nc.gpsimd.tensor_scalar(out=tmpc[:], in0=ctab[0][:, 0:HALF], scalar1=ctab[0][:, 512:513], scalar2=0.0, op0=ALU.mult, op1=ALU.add)
-        nc.gpsimd.tensor_scalar(out=tmps[:], in0=stab[0][:, 0:HALF], scalar1=ctab[0][:, 512:513], scalar2=0.0, op0=ALU.mult, op1=ALU.add)
-
-        bvps = psum.tile([P, 512], F32, name="bvps", tag="tp", bufs=4)
+        bvps = psum.tile([P, 512], F32, name="bvps", tag="tp", bufs=TPB)
         nc.tensor.matmul(out=bvps[:], lhsT=onesb[:], rhs=bvrow[:], start=True, stop=True)
         bvb = const.tile([P, 512], F32, name="bvb")
         nc.scalar.copy(out=bvb[:], in_=bvps[:])
+        nc.vector.tensor_copy(out=whole[:], in_=turns[:])
+        bcol = const.tile([P, 20], F32, name="bcol")
+        nc.vector.tensor_copy(out=bcol[:], in_=bps[:, 0:20])
+        nc.vector.tensor_tensor(out=turns[:], in0=turns[:], in1=whole[:], op=ALU.subtract)
+        ctab = [const.tile([P, TABW], F32, name="ctab0"), const.tile([P, HALF], F32, name="ctab1")]
+        stab = [const.tile([P, TABW], F32, name="stab0"), const.tile([P, HALF], F32, name="stab1")]
+        swap = const.tile([P, P], F32, name="swap")
+        nsin = const.tile([P, 1], F32, name="nsin")
+        tmpc = const.tile([P, HALF], F32, name="tmpc")
+        tmps = const.tile([P, HALF], F32, name="tmps")
 
-        rope_products(0)
-        w_quant(1, 0)
-        rope_products(1)
-        w_quant(1, 1)
-        x_transpose(1, 0)
-        x_evac(1, 0, "ss")
-        rope_products(2)
-        w_quant(1, 2)
-        rope_products(3)
-        nc.vector.tensor_scalar(out=nsin[:], in0=stab[0][:, 512:513], scalar1=-1.0, scalar2=None, op0=ALU.mult)
-        nc.vector.scalar_tensor_tensor(
-            out=ctab[1][:], in0=stab[0][:, 0:HALF], scalar=nsin[:, 0:1], in1=tmpc[:], op0=ALU.mult, op1=ALU.add
-        )
-        nc.vector.scalar_tensor_tensor(
-            out=stab[1][:], in0=ctab[0][:, 0:HALF], scalar=stab[0][:, 512:513], in1=tmps[:], op0=ALU.mult, op1=ALU.add
-        )
-
-        for k in range(2, 16 + 4 + LAG):
-            if k == 2:
-                x_quant(1, 0)
-                x_transpose(1, 1)
-                x_evac(1, 1, "ss")
-            if k == 3:
-                x_quant(1, 1)
-                x_transpose(1, 2)
-                x_evac(1, 2, "ss")
+        def ride_along(k):
             for gc in sorted(WI_STEP):
                 if WI_STEP[gc] == k:
                     w_interleave(gc[0], gc[1])
@@ -356,28 +292,82 @@ def tile_qwenattention_pa_kernel(tc, hidden_states, Wq, bq, Wk, bk, Wv, bv, out_
                         nxt = late_loads[0]
                         late_loads.remove(nxt)
                         load_w(nxt[0], nxt[1])
-            if k in (2, 3, 4) and late_loads:
-                nxt = late_loads[0]
-                late_loads.remove(nxt)
-                load_w(nxt[0], nxt[1])
+
+        def quants_of(k):
+            for gc in sorted(WI_STEP):
+                if WI_STEP[gc] + 1 == k:
+                    w_quant(gc[0], gc[1])
+
+        x_transpose(0, 0)
+        x_evac(0, 0, "ss")
+        w_interleave(0, 0)
+        x_quant(0, 0)
+        w_quant(0, 0)
+        nc.vector.scalar_tensor_tensor(out=turns[:], in0=turns[:], scalar=0.5, in1=turns[:], op0=ALU.is_gt, op1=ALU.subtract)
+        x_transpose(0, 1)
+        x_evac(0, 1, "ss")
+        for n in range(4):
+            mx_pass(n, 0)
+        w_interleave(0, 1)
+        x_quant(0, 1)
+        nc.vector.tensor_copy(out=swap[:, 0:64], in_=ident[:, 64:128])
+        nc.vector.tensor_copy(out=swap[:, 64:128], in_=ident[:, 0:64])
+        x_transpose(0, 2)
+        x_evac(0, 2, "ss")
+        w_quant(0, 1)
+        for n in range(4):
+            mx_pass(n, 1)
+        w_interleave(0, 2)
+        x_quant(0, 2)
+        w_quant(0, 2)
+        x_transpose(1, 0)
+        nc.scalar.activation(out=ctab[0][:], in_=turns[:, 0, :], func=ACT.Sin, scale=sgn[:, 0:1])
+        nc.scalar.activation(out=stab[0][:], in_=turns[:, 1, :], func=ACT.Sin, scale=sgn[:, 1:2])
+        for n in range(4):
+            mx_pass(n, 2)
+        x_evac(1, 0, "ss")
+        x_transpose(1, 1)
+        x_evac(1, 1, "ss")
+        rope_products(0)
+        x_quant(1, 0)
+        x_transpose(1, 2)
+        x_evac(1, 2, "ss")
+        rope_products(1)
+        x_quant(1, 1)
+        nc.vector.tensor_scalar(out=tmpc[:], in0=ctab[0][:, 0:HALF], scalar1=ctab[0][:, 512:513], scalar2=None, op0=ALU.mult)
+        nc.vector.tensor_scalar(out=tmps[:], in0=stab[0][:, 0:HALF], scalar1=ctab[0][:, 512:513], scalar2=None, op0=ALU.mult)
+        nc.vector.tensor_scalar(out=nsin[:], in0=stab[0][:, 512:513], scalar1=-1.0, scalar2=None, op0=ALU.mult)
+        x_quant(1, 2)
+        ride_along(1)
+        rope_products(2)
+        nc.vector.scalar_tensor_tensor(
+            out=ctab[1][:], in0=stab[0][:, 0:HALF], scalar=nsin[:, 0:1], in1=tmpc[:], op0=ALU.mult, op1=ALU.add
+        )
+        nc.vector.scalar_tensor_tensor(
+            out=stab[1][:], in0=ctab[0][:, 0:HALF], scalar=stab[0][:, 512:513], in1=tmps[:], op0=ALU.mult, op1=ALU.add
+        )
+        rope_products(3)
+
+        def finish_pair(j):
+            for n in (2 * j, 2 * j + 1):
+                turn_and_add(n)
+                y_evac(n)
+
+        for j in range(0, 2 - LAG):
+            finish_pair(j)
+        for k in range(2, 16 + 4 + LAG):
+            ride_along(k)
             if k < 16:
                 for n in (2 * k, 2 * k + 1):
                     for c in range(PASSES):
                         mx_pass(n, c)
                 rope_products(2 * k)
-                if k == 3:
-                    x_quant(1, 2)
-                for gc in sorted(WI_STEP):
-                    if WI_STEP[gc] + 1 == k:
-                        w_quant(gc[0], gc[1])
+                quants_of(k)
                 rope_products(2 * k + 1)
             elif k < 20:
                 for vb in (2 * (k - 16), 2 * (k - 16) + 1):
                     for c in range(PASSES):
                         v_pass(vb, c)
                     v_finish(vb)
-            j = k - LAG
-            if j < 16:
-                for n in (2 * j, 2 * j + 1):
-                    turn_and_add(n)
-                    y_evac(n)
+            if k - LAG < 16:
+                finish_pair(k - LAG)

@@ -124,8 +124,8 @@ def tile_qwenattention_pa_kernel(tc, hidden_states, Wq, bq, Wk, bk, Wv, bv, out_
         def w_interleave(g, c):
             wg[(g, c)] = work.tile([P, 512, 4], BF16, name="wg", tag="wg", bufs=4, align_bytes=64)
             for eng, n0, n1 in WI_PLAN.get((g, c), WI_DEFAULT[c]):
-                dst = wg[(g, c)][:, n0:n1, :]
-                src = wraw[(g, c)][:, :, n0:n1].rearrange("p j n -> p n j")
+                dst = wg[(g, c)][:, n0:n1, :].rearrange("p (m i) j -> p m j i", i=4)
+                src = wraw[(g, c)][:, :, n0:n1].rearrange("p j (m i) -> p m j i", i=4)
                 if eng == "v":
                     nc.vector.tensor_copy(out=dst, in_=src)
                 elif eng == "s":

@@ -22,6 +22,9 @@ HALF = 512
 TABW = 514
 MXB = 4
 TPB = 4
+UWB = 8
+BATCHES = [[4, 5], [6, 7]] + [list(range(n, n + 4)) for n in range(8, 32, 4)]
+VB_TURN = 1
 LAG = 1
 
 QUADS = [(0, 0), (0, 1), (1, 0), (1, 1), (2, 0), (2, 1), (3, 0), (3, 1)]
@@ -30,6 +33,7 @@ WI_PLAN = {
     (0, 0): [("v", 0, 512)],
     (0, 1): [("s", 0, 512)],
     (0, 2): [("s", 0, 192), ("v", 192, 512)],
+    (1, 2): [("v", 0, 256), ("s", 256, 512)],
 }
 WI_DEFAULT = [[("s", 0, 256), ("s", 256, 512)], [("s", 0, 256), ("s", 256, 512)], [("s", 0, 256), ("s", 256, 512)]]
 
@@ -53,15 +57,17 @@ def tile_qwenattention_pa_kernel(tc, hidden_states, Wq, bq, Wk, bk, Wv, bv, out_
 
     def w_src(g, c):
         rows = slice(c * KP, (c + 1) * KP)
-        if g < 3:
-            return w2[0][rows, g * 512 : (g + 1) * 512]
-        return w2[g - 2][rows, :]
+        if g == 0:
+            return w2[1][rows, :]
+        if g == 4:
+            return w2[2][rows, :]
+        return w2[0][rows, (g - 1) * 512 : g * 512]
 
     def o_dst(g, t):
         rows = slice(t * HALF, (t + 1) * HALF)
-        if g < 3:
-            return o2[0][rows, g * 512 : (g + 1) * 512]
-        return o2[g - 2][rows, :]
+        if g == 0:
+            return o2[1][rows, :]
+        return o2[0][rows, (g - 1) * 512 : g * 512]
 
     with ExitStack() as ctx:
         const = ctx.enter_context(tc.tile_pool(name="const", bufs=1))
@@ -124,8 +130,8 @@ def tile_qwenattention_pa_kernel(tc, hidden_states, Wq, bq, Wk, bk, Wv, bv, out_
         def w_interleave(g, c):
             wg[(g, c)] = work.tile([P, 512, 4], BF16, name="wg", tag="wg", bufs=4, align_bytes=64)
             for eng, n0, n1 in WI_PLAN.get((g, c), WI_DEFAULT[c]):
-                dst = wg[(g, c)][:, n0:n1, :].rearrange("p (m i) j -> p m j i", i=4)
-                src = wraw[(g, c)][:, :, n0:n1].rearrange("p j (m i) -> p m j i", i=4)
+                dst = wg[(g, c)][:, n0:n1, :]
+                src = wraw[(g, c)][:, :, n0:n1].rearrange("p j n -> p n j")
                 if eng == "v":
                     nc.vector.tensor_copy(out=dst, in_=src)
                 elif eng == "s":
@@ -161,9 +167,9 @@ def tile_qwenattention_pa_kernel(tc, hidden_states, Wq, bq, Wk, bk, Wv, bv, out_
 
         def rope_products(n):
             g, t, h = unit_of(n)
-            hd = 4 * g + h
-            ut[n] = work.tile([P, HALF], F32, name="ut", tag="ut", bufs=6)
-            wt[n] = work.tile([P, HALF], F32, name="wt", tag="wt", bufs=6)
+            hd = 12 + h if g == 0 else 4 * (g - 1) + h
+            ut[n] = work.tile([P, HALF], F32, name="ut", tag="ut", bufs=UWB)
+            wt[n] = work.tile([P, HALF], F32, name="wt", tag="wt", bufs=UWB)
             nc.vector.scalar_tensor_tensor(
                 out=ut[n][:], in0=acc[n][:], scalar=bcol[:, hd : hd + 1], in1=ctab[t][:, 0:HALF], op0=ALU.add, op1=ALU.mult
             )
@@ -202,14 +208,9 @@ def tile_qwenattention_pa_kernel(tc, hidden_states, Wq, bq, Wk, bk, Wv, bv, out_
             )
 
         def v_finish(vb):
-            t, b = vb // 4, vb % 4
-            if b % 2 == 0:
-                ystage[("v", vb // 2)] = work.tile([P, 2, 512], F32, name="vst", tag="vst", bufs=4)
-            st = ystage[("v", vb // 2)]
-            nc.vector.tensor_tensor(out=st[:, b % 2, :], in0=acc[("v", vb)][:], in1=bvb[:], op=ALU.add)
-            if b % 2 == 1:
-                rows = slice((vb - 1) * P, (vb + 1) * P)
-                nc.sync.dma_start(out=o2[2][rows, :].rearrange("(b p) n -> p b n", p=P), in_=st[:])
+            st = work.tile([P, 512], F32, name="vst", tag="vst", bufs=8)
+            nc.vector.tensor_tensor(out=st[:], in0=acc[("v", vb)][:], in1=bvb[:], op=ALU.add)
+            nc.sync.dma_start(out=o2[2][vb * P : (vb + 1) * P, :], in_=st[:])
 
         browb = const.tile([P, P], BF16, name="browb")
         nc.vector.memset(browb[:], 0.0)
@@ -298,20 +299,26 @@ def tile_qwenattention_pa_kernel(tc, hidden_states, Wq, bq, Wk, bk, Wv, bv, out_
                 if WI_STEP[gc] + 1 == k:
                     w_quant(gc[0], gc[1])
 
+        nc.vector.scalar_tensor_tensor(out=turns[:], in0=turns[:], scalar=0.5, in1=turns[:], op0=ALU.is_gt, op1=ALU.subtract)
         x_transpose(0, 0)
         x_evac(0, 0, "ss")
+        nc.scalar.activation(out=ctab[0][:], in_=turns[:, 0, :], func=ACT.Sin, scale=sgn[:, 0:1])
+        nc.scalar.activation(out=stab[0][:], in_=turns[:, 1, :], func=ACT.Sin, scale=sgn[:, 1:2])
         w_interleave(0, 0)
         x_quant(0, 0)
         w_quant(0, 0)
-        nc.vector.scalar_tensor_tensor(out=turns[:], in0=turns[:], scalar=0.5, in1=turns[:], op0=ALU.is_gt, op1=ALU.subtract)
         x_transpose(0, 1)
         x_evac(0, 1, "ss")
         for n in range(4):
             mx_pass(n, 0)
         w_interleave(0, 1)
+        nc.vector.tensor_scalar(out=tmpc[:], in0=ctab[0][:, 0:HALF], scalar1=ctab[0][:, 512:513], scalar2=None, op0=ALU.mult)
+        nc.vector.tensor_scalar(out=tmps[:], in0=stab[0][:, 0:HALF], scalar1=ctab[0][:, 512:513], scalar2=None, op0=ALU.mult)
+        nc.vector.tensor_scalar(out=nsin[:], in0=stab[0][:, 512:513], scalar1=-1.0, scalar2=None, op0=ALU.mult)
         x_quant(0, 1)
-        nc.vector.tensor_copy(out=swap[:, 0:64], in_=ident[:, 64:128])
-        nc.vector.tensor_copy(out=swap[:, 64:128], in_=ident[:, 0:64])
+        nc.vector.scalar_tensor_tensor(
+            out=ctab[1][:], in0=stab[0][:, 0:HALF], scalar=nsin[:, 0:1], in1=tmpc[:], op0=ALU.mult, op1=ALU.add
+        )
         x_transpose(0, 2)
         x_evac(0, 2, "ss")
         w_quant(0, 1)
@@ -321,10 +328,13 @@ def tile_qwenattention_pa_kernel(tc, hidden_states, Wq, bq, Wk, bk, Wv, bv, out_
         x_quant(0, 2)
         w_quant(0, 2)
         x_transpose(1, 0)
-        nc.scalar.activation(out=ctab[0][:], in_=turns[:, 0, :], func=ACT.Sin, scale=sgn[:, 0:1])
-        nc.scalar.activation(out=stab[0][:], in_=turns[:, 1, :], func=ACT.Sin, scale=sgn[:, 1:2])
         for n in range(4):
             mx_pass(n, 2)
+        nc.vector.scalar_tensor_tensor(
+            out=stab[1][:], in0=ctab[0][:, 0:HALF], scalar=stab[0][:, 512:513], in1=tmps[:], op0=ALU.mult, op1=ALU.add
+        )
+        nc.vector.tensor_copy(out=swap[:, 0:64], in_=ident[:, 64:128])
+        nc.vector.tensor_copy(out=swap[:, 64:128], in_=ident[:, 0:64])
         x_evac(1, 0, "ss")
         x_transpose(1, 1)
         x_evac(1, 1, "ss")
@@ -334,40 +344,34 @@ def tile_qwenattention_pa_kernel(tc, hidden_states, Wq, bq, Wk, bk, Wv, bv, out_
         x_evac(1, 2, "ss")
         rope_products(1)
         x_quant(1, 1)
-        nc.vector.tensor_scalar(out=tmpc[:], in0=ctab[0][:, 0:HALF], scalar1=ctab[0][:, 512:513], scalar2=None, op0=ALU.mult)
-        nc.vector.tensor_scalar(out=tmps[:], in0=stab[0][:, 0:HALF], scalar1=ctab[0][:, 512:513], scalar2=None, op0=ALU.mult)
-        nc.vector.tensor_scalar(out=nsin[:], in0=stab[0][:, 512:513], scalar1=-1.0, scalar2=None, op0=ALU.mult)
         x_quant(1, 2)
         ride_along(1)
         rope_products(2)
-        nc.vector.scalar_tensor_tensor(
-            out=ctab[1][:], in0=stab[0][:, 0:HALF], scalar=nsin[:, 0:1], in1=tmpc[:], op0=ALU.mult, op1=ALU.add
-        )
-        nc.vector.scalar_tensor_tensor(
-            out=stab[1][:], in0=ctab[0][:, 0:HALF], scalar=stab[0][:, 512:513], in1=tmps[:], op0=ALU.mult, op1=ALU.add
-        )
         rope_products(3)
 
-        def finish_pair(j):
-            for n in (2 * j, 2 * j + 1):
+        def finish(units):
+            for n in units:
                 turn_and_add(n)
+            for n in units:
                 y_evac(n)
 
-        for j in range(0, 2 - LAG):
-            finish_pair(j)
-        for k in range(2, 16 + 4 + LAG):
-            ride_along(k)
-            if k < 16:
-                for n in (2 * k, 2 * k + 1):
-                    for c in range(PASSES):
-                        mx_pass(n, c)
-                rope_products(2 * k)
-                quants_of(k)
-                rope_products(2 * k + 1)
-            elif k < 20:
-                for vb in (2 * (k - 16), 2 * (k - 16) + 1):
-                    for c in range(PASSES):
-                        v_pass(vb, c)
-                    v_finish(vb)
-            if k - LAG < 16:
-                finish_pair(k - LAG)
+        batches = [[0, 1], [2, 3]] + BATCHES
+        finish(batches[0])
+        for i in range(2, len(batches)):
+            units = batches[i]
+            for k in sorted(set([n // 2 for n in units])):
+                ride_along(k)
+            for n in units:
+                for c in range(PASSES):
+                    mx_pass(n, c)
+            for n in units:
+                rope_products(n)
+                if n % 2 == 0:
+                    quants_of(n // 2)
+            finish(batches[i - 1])
+        for vb in range(8):
+            for c in range(PASSES):
+                v_pass(vb, c)
+            v_finish(vb)
+            if vb == VB_TURN:
+                finish(batches[-1])

@@ -37,11 +37,11 @@ WI_PLAN = {
 }
 WI_DEFAULT = [[("s", 0, 256), ("s", 256, 512)], [("s", 0, 256), ("s", 256, 512)], [("s", 0, 256), ("s", 256, 512)]]
 
+G_BURST = {13: 2, 21: 3, 29: 4}
+G_FIRST_UNIT = 6
+
 WI_STEP = {
     (1, 0): 1, (1, 1): 2, (1, 2): 2,
-    (2, 0): 4, (2, 1): 5, (2, 2): 6,
-    (3, 0): 8, (3, 1): 9, (3, 2): 10,
-    (4, 0): 12, (4, 1): 13, (4, 2): 14,
 }
 
 
@@ -128,7 +128,10 @@ def tile_qwenattention_pa_kernel(tc, hidden_states, Wq, bq, Wk, bk, Wv, bv, out_
             )
 
         def w_interleave(g, c):
-            wg[(g, c)] = work.tile([P, 512, 4], BF16, name="wg", tag="wg", bufs=4, align_bytes=64)
+            if (g, c) == (1, 2):
+                wg[(g, c)] = work.tile([P, 512, 4], BF16, name="wgg0", tag="wgg0", bufs=1, align_bytes=64)
+            else:
+                wg[(g, c)] = work.tile([P, 512, 4], BF16, name="wg", tag="wg", bufs=3, align_bytes=64)
             for eng, n0, n1 in WI_PLAN.get((g, c), WI_DEFAULT[c]):
                 dst = wg[(g, c)][:, n0:n1, :]
                 src = wraw[(g, c)][:, :, n0:n1].rearrange("p j n -> p n j")
@@ -138,6 +141,15 @@ def tile_qwenattention_pa_kernel(tc, hidden_states, Wq, bq, Wk, bk, Wv, bv, out_
                     nc.scalar.copy(out=dst, in_=src)
                 else:
                     nc.gpsimd.tensor_scalar(out=dst, in0=src, scalar1=1.0, scalar2=0.0, op0=ALU.mult, op1=ALU.add)
+
+        def g_interleave(g, c):
+            wg[(g, c)] = work.tile([P, 512, 4], BF16, name="wgg%d" % c, tag="wgg%d" % c, bufs=1, align_bytes=64)
+            src = wraw[(g, c)][:].rearrange("p j n -> p n j")
+            nc.gpsimd.tensor_scalar(out=wg[(g, c)][:], in0=src, scalar1=1.0, scalar2=0.0, op0=ALU.mult, op1=ALU.add)
+            if late_loads:
+                nxt = late_loads[0]
+                late_loads.remove(nxt)
+                load_w(nxt[0], nxt[1])
 
         def w_quant(g, c):
             wq[(g, c)] = const.tile([P, 512], U32, name="wq%d%d" % (g, c), align_bytes=64)
@@ -208,7 +220,7 @@ def tile_qwenattention_pa_kernel(tc, hidden_states, Wq, bq, Wk, bk, Wv, bv, out_
             )
 
         def v_finish(vb):
-            st = work.tile([P, 512], F32, name="vst", tag="vst", bufs=8)
+            st = work.tile([P, 512], F32, name="ut", tag="ut", bufs=UWB)
             nc.vector.tensor_tensor(out=st[:], in0=acc[("v", vb)][:], in1=bvb[:], op=ALU.add)
             nc.sync.dma_start(out=o2[2][vb * P : (vb + 1) * P, :], in_=st[:])
 
@@ -368,6 +380,15 @@ def tile_qwenattention_pa_kernel(tc, hidden_states, Wq, bq, Wk, bk, Wv, bv, out_
                 rope_products(n)
                 if n % 2 == 0:
                     quants_of(n // 2)
+                if n == G_FIRST_UNIT:
+                    for c in range(PASSES):
+                        g_interleave(2, c)
+                if n in G_BURST:
+                    for c in (2, 1, 0):
+                        w_quant(G_BURST[n], c)
+                    if G_BURST[n] < 4:
+                        for c in range(PASSES):
+                            g_interleave(G_BURST[n] + 1, c)
             finish(batches[i - 1])
         for vb in range(8):
             for c in range(PASSES):

@@ -22,9 +22,9 @@ HALF = 512
 TABW = 514
 MXB = 4
 TPB = 4
-UWB = 8
+UWB = 4
 BATCHES = [[4, 5], [6, 7]] + [list(range(n, n + 4)) for n in range(8, 32, 4)]
-VB_TURN = 1
+VB_TURN = 2
 LAG = 1
 
 QUADS = [(0, 0), (0, 1), (1, 0), (1, 1), (2, 0), (2, 1), (3, 0), (3, 1)]
@@ -37,8 +37,12 @@ WI_PLAN = {
 }
 WI_DEFAULT = [[("s", 0, 256), ("s", 256, 512)], [("s", 0, 256), ("s", 256, 512)], [("s", 0, 256), ("s", 256, 512)]]
 
-G_BURST = {13: 2, 21: 3, 29: 4}
-G_FIRST_UNIT = 6
+WGB = [2, 2, 1]
+BURST = {12: 2, 20: 3, 28: 4}
+G_ADD = [4, 6, 8, 10, 12, 14]
+G_PIECES = {6: [(2, 2, 0), (2, 2, 1)], 13: [(3, 2, 0), (3, 2, 1)], 21: [(4, 2, 0), (4, 2, 1)]}
+S_PIECES = {4: [(2, 0, 0), (2, 0, 1)], 5: [(2, 1, 0), (2, 1, 1)], 6: [(3, 0, 0), (3, 0, 1)], 7: [(3, 1, 0), (3, 1, 1)], 8: [(4, 0, 0), (4, 0, 1)], 9: [(4, 1, 0), (4, 1, 1)]}
+LOAD_AFTER = {(1, 0): (3, 2), (1, 1): (4, 0), (1, 2): (4, 1), (2, 0): (4, 2)}
 
 WI_STEP = {
     (1, 0): 1, (1, 1): 2, (1, 2): 2,
@@ -89,6 +93,8 @@ def tile_qwenattention_pa_kernel(tc, hidden_states, Wq, bq, Wk, bk, Wv, bv, out_
         wt = {}
         ybank = {}
         ystage = {}
+        pieces_done = {}
+        staged = {}
 
         def load_x(t, c):
             xraw[(t, c)] = const.tile([P, 4, KP], BF16, name="xraw%d%d" % (t, c))
@@ -127,29 +133,49 @@ def tile_qwenattention_pa_kernel(tc, hidden_states, Wq, bq, Wk, bk, Wv, bv, out_
                 out=xq[(t, c)][:].bitcast(E5X4), scales=xs[(t, c)][:], in_=xg[(t, c)][:].rearrange("p r t -> p (r t)")
             )
 
-        def w_interleave(g, c):
-            if (g, c) == (1, 2):
-                wg[(g, c)] = work.tile([P, 512, 4], BF16, name="wgg0", tag="wgg0", bufs=1, align_bytes=64)
-            else:
-                wg[(g, c)] = work.tile([P, 512, 4], BF16, name="wg", tag="wg", bufs=3, align_bytes=64)
-            for eng, n0, n1 in WI_PLAN.get((g, c), WI_DEFAULT[c]):
-                dst = wg[(g, c)][:, n0:n1, :]
-                src = wraw[(g, c)][:, :, n0:n1].rearrange("p j n -> p n j")
-                if eng == "v":
-                    nc.vector.tensor_copy(out=dst, in_=src)
-                elif eng == "s":
-                    nc.scalar.copy(out=dst, in_=src)
+        def split_views(g, c, n0, n1):
+            views = []
+            while n0 < n1:
+                base = n0 - n0 % 256
+                two = wraw[(g, c)][:, :, base : base + 256].rearrange("p j (hh s i) -> p hh s i j", hh=2, s=2)
+                if n0 % 256 == 0 and n1 - n0 >= 256:
+                    wid = 256
+                    views.append((wg[(g, c)][:, n0 : n0 + wid, :].rearrange("p (s hh i) j -> p hh s i j", s=2, hh=2), two))
+                elif n0 % 128 == 0 and n1 - n0 >= 128:
+                    wid = 128
+                    views.append((wg[(g, c)][:, n0 : n0 + wid, :].rearrange("p (hh i) j -> p hh i j", hh=2), two[:, :, (n0 - base) // 128]))
                 else:
-                    nc.gpsimd.tensor_scalar(out=dst, in0=src, scalar1=1.0, scalar2=0.0, op0=ALU.mult, op1=ALU.add)
+                    wid = 64
+                    views.append((wg[(g, c)][:, n0 : n0 + wid, :], two[:, (n0 % 128) // 64, (n0 - base) // 128]))
+                n0 += wid
+            return views
 
-        def g_interleave(g, c):
-            wg[(g, c)] = work.tile([P, 512, 4], BF16, name="wgg%d" % c, tag="wgg%d" % c, bufs=1, align_bytes=64)
-            src = wraw[(g, c)][:].rearrange("p j n -> p n j")
-            nc.gpsimd.tensor_scalar(out=wg[(g, c)][:], in0=src, scalar1=1.0, scalar2=0.0, op0=ALU.mult, op1=ALU.add)
-            if late_loads:
-                nxt = late_loads[0]
-                late_loads.remove(nxt)
-                load_w(nxt[0], nxt[1])
+        def w_interleave(g, c):
+            wg[(g, c)] = work.tile([P, 512, 4], BF16, name="wg%d" % c, tag="wg%d" % c, bufs=WGB[c], align_bytes=64)
+            for eng, n0, n1 in WI_PLAN.get((g, c), WI_DEFAULT[c]):
+                for dst, src in split_views(g, c, n0, n1):
+                    if eng == "v":
+                        nc.vector.tensor_copy(out=dst, in_=src)
+                    else:
+                        nc.scalar.copy(out=dst, in_=src)
+
+        def piece(eng, g, c, q):
+            if (g, c) not in wg:
+                wg[(g, c)] = work.tile([P, 512, 4], BF16, name="wg%d" % c, tag="wg%d" % c, bufs=WGB[c], align_bytes=64)
+                pieces_done[(g, c)] = 0
+            cols = slice(256 * q, 256 * (q + 1))
+            if g == 4:
+                views = [(wg[(g, c)][:, cols, :], wraw[(g, c)][:, :, cols].rearrange("p j n -> p n j"))]
+            else:
+                views = split_views(g, c, 256 * q, 256 * (q + 1))
+            for dst, src in views:
+                if eng == "g":
+                    nc.gpsimd.tensor_scalar(out=dst, in0=src, scalar1=1.0, scalar2=0.0, op0=ALU.mult, op1=ALU.add)
+                else:
+                    nc.scalar.copy(out=dst, in_=src)
+            pieces_done[(g, c)] += 1
+            if pieces_done[(g, c)] == 2 and (g, c) in LOAD_AFTER:
+                load_w(LOAD_AFTER[(g, c)][0], LOAD_AFTER[(g, c)][1])
 
         def w_quant(g, c):
             wq[(g, c)] = const.tile([P, 512], U32, name="wq%d%d" % (g, c), align_bytes=64)
@@ -179,29 +205,45 @@ def tile_qwenattention_pa_kernel(tc, hidden_states, Wq, bq, Wk, bk, Wv, bv, out_
 
         def rope_products(n):
             g, t, h = unit_of(n)
-            hd = 12 + h if g == 0 else 4 * (g - 1) + h
-            ut[n] = work.tile([P, HALF], F32, name="ut", tag="ut", bufs=UWB)
-            wt[n] = work.tile([P, HALF], F32, name="wt", tag="wt", bufs=UWB)
+            s = h % 2
+            col = 8 * s + (6 + h // 2 if g == 0 else 2 * (g - 1) + h // 2)
+            if s == 0:
+                ut[n // 2] = work.tile([P, 2, HALF], F32, name="ut", tag="ut", bufs=UWB)
+                wt[n // 2] = work.tile([P, 2, HALF], F32, name="wt", tag="wt", bufs=UWB)
+            sines = stab if s == 0 else nstab
             nc.vector.scalar_tensor_tensor(
-                out=ut[n][:], in0=acc[n][:], scalar=bcol[:, hd : hd + 1], in1=ctab[t][:, 0:HALF], op0=ALU.add, op1=ALU.mult
+                out=ut[n // 2][:, s, :], in0=acc[n][:], scalar=bcol[:, col : col + 1], in1=ctab[t][:, 0:HALF], op0=ALU.add, op1=ALU.mult
             )
             nc.vector.scalar_tensor_tensor(
-                out=wt[n][:], in0=acc[n][:], scalar=bcol[:, hd : hd + 1], in1=stab[t][:, 0:HALF], op0=ALU.add, op1=ALU.mult
+                out=wt[n // 2][:, 1 - s, :], in0=acc[n][:], scalar=bcol[:, col : col + 1], in1=sines[t][:, 0:HALF], op0=ALU.add, op1=ALU.mult
             )
+            if s == 1 and n // 2 in G_ADD:
+                nc.gpsimd.tensor_tensor(
+                    out=ut[n // 2][:].rearrange("p a r -> p (a r)"),
+                    in0=ut[n // 2][:].rearrange("p a r -> p (a r)"),
+                    in1=wt[n // 2][:].rearrange("p a r -> p (a r)"),
+                    op=ALU.add,
+                )
 
         def turn_and_add(n):
             ybank[n] = psum.tile([P, 4, P], F32, name="yb", tag="tp", bufs=TPB)
             for b in range(4):
                 cols = slice(b * P, (b + 1) * P)
-                nc.tensor.matmul(out=ybank[n][:, b, :], lhsT=ut[n][:, cols], rhs=ident[:], is_transpose=True, start=True, stop=False)
-                nc.tensor.matmul(out=ybank[n][:, b, :], lhsT=wt[n][:, cols], rhs=swap[:], is_transpose=True, start=False, stop=True)
+                if n // 2 in G_ADD:
+                    nc.tensor.transpose(ybank[n][:, b, :], ut[n // 2][:, n % 2, cols], ident[:])
+                else:
+                    nc.tensor.matmul(out=ybank[n][:, b, :], lhsT=ut[n // 2][:, n % 2, cols], rhs=ident[:], is_transpose=True, start=True, stop=False)
+                    nc.tensor.matmul(out=ybank[n][:, b, :], lhsT=wt[n // 2][:, n % 2, cols], rhs=ident[:], is_transpose=True, start=False, stop=True)
 
         def y_evac(n):
             g, t, h = unit_of(n)
-            if h == 0:
+            if (g, t) not in ystage:
                 ystage[(g, t)] = work.tile([P, 4, 512], F32, name="yst", tag="yst", bufs=3)
-            nc.scalar.copy(out=ystage[(g, t)][:, :, h * P : (h + 1) * P], in_=ybank[n][:])
-            if h == 3:
+                staged[(g, t)] = 0
+            dst = ystage[(g, t)][:].rearrange("p b (q hh s i) -> p b q hh s i", q=2, hh=2, s=2)[:, :, h // 2, :, h % 2, :]
+            nc.scalar.copy(out=dst, in_=ybank[n][:].rearrange("p b (hh i) -> p b hh i", hh=2))
+            staged[(g, t)] += 1
+            if staged[(g, t)] == 4:
                 nc.sync.dma_start(out=o_dst(g, t).rearrange("(b p) n -> p b n", p=P), in_=ystage[(g, t)][:])
 
         def v_pass(vb, c):
@@ -220,7 +262,10 @@ def tile_qwenattention_pa_kernel(tc, hidden_states, Wq, bq, Wk, bk, Wv, bv, out_
             )
 
         def v_finish(vb):
-            st = work.tile([P, 512], F32, name="ut", tag="ut", bufs=UWB)
+            if vb % 2 == 0:
+                st = work.tile([P, 512], F32, name="ut", tag="ut", bufs=UWB)
+            else:
+                st = work.tile([P, 512], F32, name="wt", tag="wt", bufs=UWB)
             nc.vector.tensor_tensor(out=st[:], in0=acc[("v", vb)][:], in1=bvb[:], op=ALU.add)
             nc.sync.dma_start(out=o2[2][vb * P : (vb + 1) * P, :], in_=st[:])
 
@@ -228,9 +273,14 @@ def tile_qwenattention_pa_kernel(tc, hidden_states, Wq, bq, Wk, bk, Wv, bv, out_
         nc.vector.memset(browb[:], 0.0)
         bvrow = const.tile([P, 512], BF16, name="bvrow")
         nc.vector.memset(bvrow[:], 0.0)
-        nc.scalar.dma_start(out=browb[0:12, :], in_=bq)
-        nc.scalar.dma_start(out=browb[12:16, :], in_=bk)
-        nc.scalar.dma_start(out=browb[16:20, :], in_=bv)
+        for s in range(2):
+            half = slice(64 * s, 64 * (s + 1))
+            nc.scalar.dma_start(
+                out=browb[8 * s : 8 * s + 6, :].rearrange("q (hh i) -> q hh i", hh=2), in_=bq[:, half].rearrange("(q hh) i -> q hh i", hh=2)
+            )
+            nc.scalar.dma_start(
+                out=browb[8 * s + 6 : 8 * s + 8, :].rearrange("q (hh i) -> q hh i", hh=2), in_=bk[:, half].rearrange("(q hh) i -> q hh i", hh=2)
+            )
         nc.scalar.dma_start(out=bvrow[0:1, :], in_=bv.rearrange("(o v) h -> o (v h)", o=1))
         for c in range(PASSES):
             load_x(0, c)
@@ -239,7 +289,6 @@ def tile_qwenattention_pa_kernel(tc, hidden_states, Wq, bq, Wk, bk, Wv, bv, out_
             load_x(1, c)
         for g, c in [(1, 0), (1, 1), (1, 2), (2, 0), (2, 1)]:
             load_w(g, c)
-        late_loads = [(2, 2), (3, 0), (3, 1), (3, 2), (4, 0), (4, 1), (4, 2)]
 
         ident = const.tile([P, P], F32, name="ident")
         make_identity(nc, ident[:])
@@ -255,7 +304,6 @@ def tile_qwenattention_pa_kernel(tc, hidden_states, Wq, bq, Wk, bk, Wv, bv, out_
         nc.vector.tensor_scalar(out=grow[:, 0:1], in0=one[:], scalar1=1.0 / (2.0 * PI), scalar2=None, op0=ALU.mult)
         onesb = const.tile([P, P], BF16, name="onesb")
         phase = const.tile([P, 2], F32, name="phase")
-        sgn = const.tile([P, 2], F32, name="sgn")
         for s in (1, 2, 4, 8, 16, 32):
             nc.vector.tensor_scalar(
                 out=grow[:, s : 2 * s], in0=grow[:, 0:s], scalar1=10000.0 ** (-s / 64.0), scalar2=None, op0=ALU.mult
@@ -266,9 +314,6 @@ def tile_qwenattention_pa_kernel(tc, hidden_states, Wq, bq, Wk, bk, Wv, bv, out_
         nc.vector.memset(onesb[:], 1.0)
         nc.vector.memset(phase[:, 0:1], 0.25)
         nc.vector.memset(phase[:, 1:2], 0.0)
-        nc.vector.tensor_scalar(out=sgn[:, 0:1], in0=one[:], scalar1=-2.0 * PI, scalar2=None, op0=ALU.mult)
-        nc.vector.tensor_scalar(out=sgn[0:64, 1:2], in0=one[0:64, :], scalar1=-2.0 * PI, scalar2=None, op0=ALU.mult)
-        nc.vector.tensor_scalar(out=sgn[64:128, 1:2], in0=one[64:128, :], scalar1=2.0 * PI, scalar2=None, op0=ALU.mult)
         gcol = const.tile([P, 1], F32, name="gcol")
         nc.vector.tensor_copy(out=gcol[:], in_=gps[:, 0:1])
 
@@ -287,12 +332,12 @@ def tile_qwenattention_pa_kernel(tc, hidden_states, Wq, bq, Wk, bk, Wv, bv, out_
         bvb = const.tile([P, 512], F32, name="bvb")
         nc.scalar.copy(out=bvb[:], in_=bvps[:])
         nc.vector.tensor_copy(out=whole[:], in_=turns[:])
-        bcol = const.tile([P, 20], F32, name="bcol")
-        nc.vector.tensor_copy(out=bcol[:], in_=bps[:, 0:20])
+        bcol = const.tile([P, 16], F32, name="bcol")
+        nc.vector.tensor_copy(out=bcol[:], in_=bps[:, 0:16])
         nc.vector.tensor_tensor(out=turns[:], in0=turns[:], in1=whole[:], op=ALU.subtract)
         ctab = [const.tile([P, TABW], F32, name="ctab0"), const.tile([P, HALF], F32, name="ctab1")]
         stab = [const.tile([P, TABW], F32, name="stab0"), const.tile([P, HALF], F32, name="stab1")]
-        swap = const.tile([P, P], F32, name="swap")
+        nstab = [const.tile([P, HALF], F32, name="nstab0"), const.tile([P, HALF], F32, name="nstab1")]
         nsin = const.tile([P, 1], F32, name="nsin")
         tmpc = const.tile([P, HALF], F32, name="tmpc")
         tmps = const.tile([P, HALF], F32, name="tmps")
@@ -301,10 +346,7 @@ def tile_qwenattention_pa_kernel(tc, hidden_states, Wq, bq, Wk, bk, Wv, bv, out_
             for gc in sorted(WI_STEP):
                 if WI_STEP[gc] == k:
                     w_interleave(gc[0], gc[1])
-                    if late_loads:
-                        nxt = late_loads[0]
-                        late_loads.remove(nxt)
-                        load_w(nxt[0], nxt[1])
+                    load_w(LOAD_AFTER[gc][0], LOAD_AFTER[gc][1])
 
         def quants_of(k):
             for gc in sorted(WI_STEP):
@@ -314,9 +356,10 @@ def tile_qwenattention_pa_kernel(tc, hidden_states, Wq, bq, Wk, bk, Wv, bv, out_
         nc.vector.scalar_tensor_tensor(out=turns[:], in0=turns[:], scalar=0.5, in1=turns[:], op0=ALU.is_gt, op1=ALU.subtract)
         x_transpose(0, 0)
         x_evac(0, 0, "ss")
-        nc.scalar.activation(out=ctab[0][:], in_=turns[:, 0, :], func=ACT.Sin, scale=sgn[:, 0:1])
-        nc.scalar.activation(out=stab[0][:], in_=turns[:, 1, :], func=ACT.Sin, scale=sgn[:, 1:2])
+        nc.scalar.activation(out=ctab[0][:], in_=turns[:, 0, :], func=ACT.Sin, scale=-2.0 * PI)
+        nc.scalar.activation(out=stab[0][:], in_=turns[:, 1, :], func=ACT.Sin, scale=-2.0 * PI)
         w_interleave(0, 0)
+        load_w(2, 2)
         x_quant(0, 0)
         w_quant(0, 0)
         x_transpose(0, 1)
@@ -324,6 +367,7 @@ def tile_qwenattention_pa_kernel(tc, hidden_states, Wq, bq, Wk, bk, Wv, bv, out_
         for n in range(4):
             mx_pass(n, 0)
         w_interleave(0, 1)
+        load_w(3, 0)
         nc.vector.tensor_scalar(out=tmpc[:], in0=ctab[0][:, 0:HALF], scalar1=ctab[0][:, 512:513], scalar2=None, op0=ALU.mult)
         nc.vector.tensor_scalar(out=tmps[:], in0=stab[0][:, 0:HALF], scalar1=ctab[0][:, 512:513], scalar2=None, op0=ALU.mult)
         nc.vector.tensor_scalar(out=nsin[:], in0=stab[0][:, 512:513], scalar1=-1.0, scalar2=None, op0=ALU.mult)
@@ -337,6 +381,7 @@ def tile_qwenattention_pa_kernel(tc, hidden_states, Wq, bq, Wk, bk, Wv, bv, out_
         for n in range(4):
             mx_pass(n, 1)
         w_interleave(0, 2)
+        load_w(3, 1)
         x_quant(0, 2)
         w_quant(0, 2)
         x_transpose(1, 0)
@@ -345,11 +390,11 @@ def tile_qwenattention_pa_kernel(tc, hidden_states, Wq, bq, Wk, bk, Wv, bv, out_
         nc.vector.scalar_tensor_tensor(
             out=stab[1][:], in0=ctab[0][:, 0:HALF], scalar=stab[0][:, 512:513], in1=tmps[:], op0=ALU.mult, op1=ALU.add
         )
-        nc.vector.tensor_copy(out=swap[:, 0:64], in_=ident[:, 64:128])
-        nc.vector.tensor_copy(out=swap[:, 64:128], in_=ident[:, 0:64])
+        nc.scalar.activation(out=nstab[0][:], in_=stab[0][:, 0:HALF], func=ACT.Copy, scale=-1.0)
         x_evac(1, 0, "ss")
         x_transpose(1, 1)
         x_evac(1, 1, "ss")
+        nc.scalar.activation(out=nstab[1][:], in_=stab[1][:], func=ACT.Copy, scale=-1.0)
         rope_products(0)
         x_quant(1, 0)
         x_transpose(1, 2)
@@ -362,9 +407,10 @@ def tile_qwenattention_pa_kernel(tc, hidden_states, Wq, bq, Wk, bk, Wv, bv, out_
         rope_products(3)
 
         def finish(units):
-            for n in units:
+            order = [n for n in units if n // 2 not in G_ADD] + [n for n in units if n // 2 in G_ADD]
+            for n in order:
                 turn_and_add(n)
-            for n in units:
+            for n in order:
                 y_evac(n)
 
         batches = [[0, 1], [2, 3]] + BATCHES
@@ -373,6 +419,8 @@ def tile_qwenattention_pa_kernel(tc, hidden_states, Wq, bq, Wk, bk, Wv, bv, out_
             units = batches[i]
             for k in sorted(set([n // 2 for n in units])):
                 ride_along(k)
+            for pc in S_PIECES.get(i, []):
+                piece("s", pc[0], pc[1], pc[2])
             for n in units:
                 for c in range(PASSES):
                     mx_pass(n, c)
@@ -380,15 +428,11 @@ def tile_qwenattention_pa_kernel(tc, hidden_states, Wq, bq, Wk, bk, Wv, bv, out_
                 rope_products(n)
                 if n % 2 == 0:
                     quants_of(n // 2)
-                if n == G_FIRST_UNIT:
-                    for c in range(PASSES):
-                        g_interleave(2, c)
-                if n in G_BURST:
-                    for c in (2, 1, 0):
-                        w_quant(G_BURST[n], c)
-                    if G_BURST[n] < 4:
-                        for c in range(PASSES):
-                            g_interleave(G_BURST[n] + 1, c)
+                for pc in G_PIECES.get(n, []):
+                    piece("g", pc[0], pc[1], pc[2])
+                if n in BURST:
+                    for c in (2, 0, 1):
+                        w_quant(BURST[n], c)
             finish(batches[i - 1])
         for vb in range(8):
             for c in range(PASSES):

@@ -24,15 +24,17 @@ MXB = 4
 TPB = 4
 UWB = 4
 BATCHES = [[4, 5], [6, 7]] + [list(range(n, n + 4)) for n in range(8, 32, 4)]
-VB_TURN = 2
+BV_BATCH = 6
+TURN_UPTO = {2: 1, 3: 2, 4: 3, 5: 5, 6: 7, 7: 9, 8: 11, 9: 13}
+V_TURNS = {2: 15}
 LAG = 1
 
 QUADS = [(0, 0), (0, 1), (1, 0), (1, 1), (2, 0), (2, 1), (3, 0), (3, 1)]
 
 WI_PLAN = {
     (0, 0): [("v", 0, 512)],
-    (0, 1): [("s", 0, 512)],
-    (0, 2): [("s", 0, 192), ("v", 192, 512)],
+    (0, 1): [("v", 0, 512)],
+    (0, 2): [("v", 0, 512)],
     (1, 2): [("v", 0, 256), ("s", 256, 512)],
 }
 WI_DEFAULT = [[("s", 0, 256), ("s", 256, 512)], [("s", 0, 256), ("s", 256, 512)], [("s", 0, 256), ("s", 256, 512)]]
@@ -323,17 +325,7 @@ def tile_qwenattention_pa_kernel(tc, hidden_states, Wq, bq, Wk, bk, Wv, bv, out_
             nc.vector.tensor_scalar(
                 out=turns[:, j, :], in0=tokf[:], scalar1=gcol[:, 0:1], scalar2=phase[:, j : j + 1], op0=ALU.mult, op1=ALU.add
             )
-        brow = const.tile([P, P], F32, name="brow")
-        nc.vector.tensor_copy(out=brow[:], in_=browb[:])
-        bps = psum.tile([P, P], F32, name="bps", tag="tp", bufs=TPB)
-        nc.tensor.transpose(bps[:], brow[:], ident[:])
-        bvps = psum.tile([P, 512], F32, name="bvps", tag="tp", bufs=TPB)
-        nc.tensor.matmul(out=bvps[:], lhsT=onesb[:], rhs=bvrow[:], start=True, stop=True)
-        bvb = const.tile([P, 512], F32, name="bvb")
-        nc.scalar.copy(out=bvb[:], in_=bvps[:])
         nc.vector.tensor_copy(out=whole[:], in_=turns[:])
-        bcol = const.tile([P, 16], F32, name="bcol")
-        nc.vector.tensor_copy(out=bcol[:], in_=bps[:, 0:16])
         nc.vector.tensor_tensor(out=turns[:], in0=turns[:], in1=whole[:], op=ALU.subtract)
         ctab = [const.tile([P, TABW], F32, name="ctab0"), const.tile([P, HALF], F32, name="ctab1")]
         stab = [const.tile([P, TABW], F32, name="stab0"), const.tile([P, HALF], F32, name="stab1")]
@@ -341,6 +333,9 @@ def tile_qwenattention_pa_kernel(tc, hidden_states, Wq, bq, Wk, bk, Wv, bv, out_
         nsin = const.tile([P, 1], F32, name="nsin")
         tmpc = const.tile([P, HALF], F32, name="tmpc")
         tmps = const.tile([P, HALF], F32, name="tmps")
+        brow = const.tile([P, P], F32, name="brow")
+        bcol = const.tile([P, 16], F32, name="bcol")
+        bvb = const.tile([P, 512], F32, name="bvb")
 
         def ride_along(k):
             for gc in sorted(WI_STEP):
@@ -353,68 +348,75 @@ def tile_qwenattention_pa_kernel(tc, hidden_states, Wq, bq, Wk, bk, Wv, bv, out_
                 if WI_STEP[gc] + 1 == k:
                     w_quant(gc[0], gc[1])
 
-        nc.vector.scalar_tensor_tensor(out=turns[:], in0=turns[:], scalar=0.5, in1=turns[:], op0=ALU.is_gt, op1=ALU.subtract)
+        nc.vector.tensor_copy(out=brow[:], in_=browb[:])
+        bps = psum.tile([P, P], F32, name="bps", tag="tp", bufs=TPB)
         x_transpose(0, 0)
+        nc.tensor.transpose(bps[:], brow[:], ident[:])
         x_evac(0, 0, "ss")
-        nc.scalar.activation(out=ctab[0][:], in_=turns[:, 0, :], func=ACT.Sin, scale=-2.0 * PI)
-        nc.scalar.activation(out=stab[0][:], in_=turns[:, 1, :], func=ACT.Sin, scale=-2.0 * PI)
+        nc.scalar.activation(out=ctab[0][:], in_=turns[:, 0, :], func=ACT.Sin, scale=2.0 * PI)
+        nc.scalar.activation(out=stab[0][:], in_=turns[:, 1, :], func=ACT.Sin, scale=2.0 * PI)
         w_interleave(0, 0)
         load_w(2, 2)
+        nc.vector.tensor_copy(out=bcol[:], in_=bps[:, 0:16])
         x_quant(0, 0)
         w_quant(0, 0)
         x_transpose(0, 1)
         x_evac(0, 1, "ss")
-        for n in range(4):
-            mx_pass(n, 0)
         w_interleave(0, 1)
         load_w(3, 0)
-        nc.vector.tensor_scalar(out=tmpc[:], in0=ctab[0][:, 0:HALF], scalar1=ctab[0][:, 512:513], scalar2=None, op0=ALU.mult)
-        nc.vector.tensor_scalar(out=tmps[:], in0=stab[0][:, 0:HALF], scalar1=ctab[0][:, 512:513], scalar2=None, op0=ALU.mult)
-        nc.vector.tensor_scalar(out=nsin[:], in0=stab[0][:, 512:513], scalar1=-1.0, scalar2=None, op0=ALU.mult)
         x_quant(0, 1)
-        nc.vector.scalar_tensor_tensor(
-            out=ctab[1][:], in0=stab[0][:, 0:HALF], scalar=nsin[:, 0:1], in1=tmpc[:], op0=ALU.mult, op1=ALU.add
-        )
+        w_quant(0, 1)
+        nc.scalar.activation(out=nstab[0][:], in_=turns[:, 1, 0:HALF], func=ACT.Sin, scale=-2.0 * PI)
         x_transpose(0, 2)
         x_evac(0, 2, "ss")
-        w_quant(0, 1)
+        for n in range(4):
+            mx_pass(n, 0)
         for n in range(4):
             mx_pass(n, 1)
         w_interleave(0, 2)
         load_w(3, 1)
         x_quant(0, 2)
         w_quant(0, 2)
-        x_transpose(1, 0)
         for n in range(4):
             mx_pass(n, 2)
-        nc.vector.scalar_tensor_tensor(
-            out=stab[1][:], in0=ctab[0][:, 0:HALF], scalar=stab[0][:, 512:513], in1=tmps[:], op0=ALU.mult, op1=ALU.add
-        )
-        nc.scalar.activation(out=nstab[0][:], in_=stab[0][:, 0:HALF], func=ACT.Copy, scale=-1.0)
+        x_transpose(1, 0)
+        nc.vector.tensor_scalar(out=tmpc[:], in0=ctab[0][:, 0:HALF], scalar1=ctab[0][:, 512:513], scalar2=None, op0=ALU.mult)
+        nc.vector.tensor_scalar(out=tmps[:], in0=stab[0][:, 0:HALF], scalar1=ctab[0][:, 512:513], scalar2=None, op0=ALU.mult)
+        nc.vector.tensor_scalar(out=nsin[:], in0=stab[0][:, 512:513], scalar1=-1.0, scalar2=None, op0=ALU.mult)
         x_evac(1, 0, "ss")
         x_transpose(1, 1)
         x_evac(1, 1, "ss")
-        nc.scalar.activation(out=nstab[1][:], in_=stab[1][:], func=ACT.Copy, scale=-1.0)
-        rope_products(0)
-        x_quant(1, 0)
         x_transpose(1, 2)
         x_evac(1, 2, "ss")
+        rope_products(0)
         rope_products(1)
-        x_quant(1, 1)
-        x_quant(1, 2)
-        ride_along(1)
         rope_products(2)
         rope_products(3)
+        x_quant(1, 0)
+        x_quant(1, 1)
+        x_quant(1, 2)
+        nc.vector.scalar_tensor_tensor(
+            out=ctab[1][:], in0=stab[0][:, 0:HALF], scalar=nsin[:, 0:1], in1=tmpc[:], op0=ALU.mult, op1=ALU.add
+        )
+        nc.vector.scalar_tensor_tensor(
+            out=stab[1][:], in0=ctab[0][:, 0:HALF], scalar=stab[0][:, 512:513], in1=tmps[:], op0=ALU.mult, op1=ALU.add
+        )
+        ride_along(1)
+        nc.scalar.activation(out=nstab[1][:], in_=stab[1][:], func=ACT.Copy, scale=-1.0)
 
-        def finish(units):
+        turned = []
+
+        def finish_upto(last):
+            units = [n for n in range(2 * len(turned), 2 * last + 2)]
             order = [n for n in units if n // 2 not in G_ADD] + [n for n in units if n // 2 in G_ADD]
             for n in order:
                 turn_and_add(n)
             for n in order:
                 y_evac(n)
+            turned.extend(units[0::2])
 
         batches = [[0, 1], [2, 3]] + BATCHES
-        finish(batches[0])
+        finish_upto(0)
         for i in range(2, len(batches)):
             units = batches[i]
             for k in sorted(set([n // 2 for n in units])):
@@ -433,10 +435,14 @@ def tile_qwenattention_pa_kernel(tc, hidden_states, Wq, bq, Wk, bk, Wv, bv, out_
                 if n in BURST:
                     for c in (2, 0, 1):
                         w_quant(BURST[n], c)
-            finish(batches[i - 1])
+            finish_upto(TURN_UPTO[i])
+            if i == BV_BATCH:
+                bvps = psum.tile([P, 512], F32, name="bvps", tag="tp", bufs=TPB)
+                nc.tensor.matmul(out=bvps[:], lhsT=onesb[:], rhs=bvrow[:], start=True, stop=True)
+                nc.scalar.copy(out=bvb[:], in_=bvps[:])
         for vb in range(8):
             for c in range(PASSES):
                 v_pass(vb, c)
             v_finish(vb)
-            if vb == VB_TURN:
-                finish(batches[-1])
+            if vb in V_TURNS:
+                finish_upto(V_TURNS[vb])

@@ -22,11 +22,11 @@ HALF = 512
 TABW = 514
 MXB = 4
 TPB = 4
-UWB = 4
+UWB = 5
 BATCHES = [[4, 5], [6, 7]] + [list(range(n, n + 4)) for n in range(8, 32, 4)]
 BV_BATCH = 6
-TURN_UPTO = {2: 1, 3: 2, 4: 3, 5: 5, 6: 7, 7: 9, 8: 11, 9: 13}
-V_TURNS = {2: 15}
+TURN_UPTO = {2: 1, 3: 2, 4: 3, 5: 4, 6: 6, 7: 8, 8: 10, 9: 12}
+V_TURNS = {0: 13, 2: 15}
 LAG = 1
 
 QUADS = [(0, 0), (0, 1), (1, 0), (1, 1), (2, 0), (2, 1), (3, 0), (3, 1)]
@@ -40,10 +40,12 @@ WI_PLAN = {
 WI_DEFAULT = [[("s", 0, 256), ("s", 256, 512)], [("s", 0, 256), ("s", 256, 512)], [("s", 0, 256), ("s", 256, 512)]]
 
 WGB = [2, 2, 1]
+BURST_ORDER = (0, 1, 2)
+G_AFTER = {12: [(3, 2, 1)], 20: [(4, 2, 1)]}
 BURST = {12: 2, 20: 3, 28: 4}
-G_ADD = [4, 6, 8, 10, 12, 14]
-G_PIECES = {6: [(2, 2, 0), (2, 2, 1)], 13: [(3, 2, 0), (3, 2, 1)], 21: [(4, 2, 0), (4, 2, 1)]}
-S_PIECES = {4: [(2, 0, 0), (2, 0, 1)], 5: [(2, 1, 0), (2, 1, 1)], 6: [(3, 0, 0), (3, 0, 1)], 7: [(3, 1, 0), (3, 1, 1)], 8: [(4, 0, 0), (4, 0, 1)], 9: [(4, 1, 0), (4, 1, 1)]}
+G_ADD = [4, 6, 7, 8, 10, 11, 12, 14, 15]
+G_PIECES = {6: [(2, 2, 0), (2, 2, 1)], 9: [(2, 1, 1)]}
+S_PIECES = {4: [(2, 0, 0), (2, 0, 1)], 5: [(2, 1, 0), (3, 0, 0)], 6: [(3, 0, 1), (3, 1, 0), (3, 1, 1)], 7: [(3, 2, 0), (4, 0, 0)], 8: [(4, 0, 1), (4, 1, 0), (4, 1, 1)], 9: [(4, 2, 0)]}
 LOAD_AFTER = {(1, 0): (3, 2), (1, 1): (4, 0), (1, 2): (4, 1), (2, 0): (4, 2)}
 
 WI_STEP = {
@@ -433,8 +435,10 @@ def tile_qwenattention_pa_kernel(tc, hidden_states, Wq, bq, Wk, bk, Wv, bv, out_
                 for pc in G_PIECES.get(n, []):
                     piece("g", pc[0], pc[1], pc[2])
                 if n in BURST:
-                    for c in (2, 0, 1):
+                    for c in BURST_ORDER:
                         w_quant(BURST[n], c)
+                for pc in G_AFTER.get(n, []):
+                    piece("g", pc[0], pc[1], pc[2])
             finish_upto(TURN_UPTO[i])
             if i == BV_BATCH:
                 bvps = psum.tile([P, 512], F32, name="bvps", tag="tp", bufs=TPB)

@@ -24,6 +24,7 @@ MXB = 4
 TPB = 4
 UWB = 5
 BATCHES = [[4, 5], [6, 7]] + [list(range(n, n + 4)) for n in range(8, 32, 4)]
+FIRST_TURN = 1
 BV_BATCH = 6
 TURN_UPTO = {2: 1, 3: 2, 4: 3, 5: 4, 6: 6, 7: 8, 8: 10, 9: 12}
 V_TURNS = {0: 13, 2: 15}
@@ -41,16 +42,16 @@ WI_DEFAULT = [[("s", 0, 256), ("s", 256, 512)], [("s", 0, 256), ("s", 256, 512)]
 
 WGB = [2, 2, 1]
 BURST_ORDER = (0, 1, 2)
-G_AFTER = {12: [(3, 2, 1)], 20: [(4, 2, 1)]}
-BURST = {12: 2, 20: 3, 28: 4}
+G_AFTER = {5: [(2, 2, 0), (2, 2, 1), (2, 1, 1)], 12: [(3, 2, 1)], 20: [(4, 2, 1)]}
+BURST = {5: 1, 12: 2, 20: 3, 28: 4}
 G_ADD = [4, 6, 7, 8, 10, 11, 12, 14, 15]
-G_PIECES = {6: [(2, 2, 0), (2, 2, 1)], 9: [(2, 1, 1)]}
+G_PIECES = {}
 S_PIECES = {4: [(2, 0, 0), (2, 0, 1)], 5: [(2, 1, 0), (3, 0, 0)], 6: [(3, 0, 1), (3, 1, 0), (3, 1, 1)], 7: [(3, 2, 0), (4, 0, 0)], 8: [(4, 0, 1), (4, 1, 0), (4, 1, 1)], 9: [(4, 2, 0)]}
 LOAD_AFTER = {(1, 0): (3, 2), (1, 1): (4, 0), (1, 2): (4, 1), (2, 0): (4, 2)}
 
-WI_STEP = {
-    (1, 0): 1, (1, 1): 2, (1, 2): 2,
-}
+WI_STEP = {}
+HEAD_S = [(1, 0, 0), (1, 0, 1), (1, 2, 1)]
+HEAD_G = [(1, 1, 0), (1, 1, 1), (1, 2, 0)]
 
 
 def tile_qwenattention_pa_kernel(tc, hidden_states, Wq, bq, Wk, bk, Wv, bv, out_0, out_1, out_2):
@@ -165,7 +166,10 @@ def tile_qwenattention_pa_kernel(tc, hidden_states, Wq, bq, Wk, bk, Wv, bv, out_
 
         def piece(eng, g, c, q):
             if (g, c) not in wg:
-                wg[(g, c)] = work.tile([P, 512, 4], BF16, name="wg%d" % c, tag="wg%d" % c, bufs=WGB[c], align_bytes=64)
+                if (g, c) == HEAD_G[0][0:2]:
+                    wg[(g, c)] = work.tile([P, 512, 4], BF16, name="xg", tag="xg", bufs=3, align_bytes=64)
+                else:
+                    wg[(g, c)] = work.tile([P, 512, 4], BF16, name="wg%d" % c, tag="wg%d" % c, bufs=WGB[c], align_bytes=64)
                 pieces_done[(g, c)] = 0
             cols = slice(256 * q, 256 * (q + 1))
             if g == 4:
@@ -375,16 +379,29 @@ def tile_qwenattention_pa_kernel(tc, hidden_states, Wq, bq, Wk, bk, Wv, bv, out_
             mx_pass(n, 0)
         for n in range(4):
             mx_pass(n, 1)
-        w_interleave(0, 2)
+        wg[(0, 2)] = work.tile([P, 512, 4], BF16, name="wg2", tag="wg2", bufs=WGB[2], align_bytes=64)
+        wq[(0, 2)] = const.tile([P, 512], U32, name="wq02", align_bytes=64)
+        ws[(0, 2)] = const.tile([P, 512], U8, name="ws02", align_bytes=64)
+        for q in range(2):
+            cols = slice(256 * q, 256 * (q + 1))
+            for dst, src in split_views(0, 2, 256 * q, 256 * (q + 1)):
+                nc.vector.tensor_copy(out=dst, in_=src)
+            if q == 0:
+                x_quant(0, 2)
+            nc.vector.quantize_mx(
+                out=wq[(0, 2)][:, cols].bitcast(E5X4), scales=ws[(0, 2)][:, cols], in_=wg[(0, 2)][:, cols, :].rearrange("p n j -> p (n j)")
+            )
         load_w(3, 1)
-        x_quant(0, 2)
-        w_quant(0, 2)
         for n in range(4):
             mx_pass(n, 2)
         x_transpose(1, 0)
-        nc.vector.tensor_scalar(out=tmpc[:], in0=ctab[0][:, 0:HALF], scalar1=ctab[0][:, 512:513], scalar2=None, op0=ALU.mult)
-        nc.vector.tensor_scalar(out=tmps[:], in0=stab[0][:, 0:HALF], scalar1=ctab[0][:, 512:513], scalar2=None, op0=ALU.mult)
+        nc.scalar.activation(out=tmpc[:], in_=ctab[0][:, 0:HALF], func=ACT.Copy, scale=ctab[0][:, 512:513])
+        nc.scalar.activation(out=tmps[:], in_=stab[0][:, 0:HALF], func=ACT.Copy, scale=ctab[0][:, 512:513])
         nc.vector.tensor_scalar(out=nsin[:], in0=stab[0][:, 512:513], scalar1=-1.0, scalar2=None, op0=ALU.mult)
+        nc.gpsimd.tensor_scalar(out=ctab[1][:], in0=stab[0][:, 0:HALF], scalar1=nsin[:, 0:1], scalar2=0.0, op0=ALU.mult, op1=ALU.add)
+        nc.gpsimd.tensor_tensor(out=ctab[1][:], in0=ctab[1][:], in1=tmpc[:], op=ALU.add)
+        nc.gpsimd.tensor_scalar(out=stab[1][:], in0=ctab[0][:, 0:HALF], scalar1=stab[0][:, 512:513], scalar2=0.0, op0=ALU.mult, op1=ALU.add)
+        nc.gpsimd.tensor_tensor(out=stab[1][:], in0=stab[1][:], in1=tmps[:], op=ALU.add)
         x_evac(1, 0, "ss")
         x_transpose(1, 1)
         x_evac(1, 1, "ss")
@@ -394,16 +411,13 @@ def tile_qwenattention_pa_kernel(tc, hidden_states, Wq, bq, Wk, bk, Wv, bv, out_
         rope_products(1)
         rope_products(2)
         rope_products(3)
-        x_quant(1, 0)
         x_quant(1, 1)
         x_quant(1, 2)
-        nc.vector.scalar_tensor_tensor(
-            out=ctab[1][:], in0=stab[0][:, 0:HALF], scalar=nsin[:, 0:1], in1=tmpc[:], op0=ALU.mult, op1=ALU.add
-        )
-        nc.vector.scalar_tensor_tensor(
-            out=stab[1][:], in0=ctab[0][:, 0:HALF], scalar=stab[0][:, 512:513], in1=tmps[:], op0=ALU.mult, op1=ALU.add
-        )
-        ride_along(1)
+        x_quant(1, 0)
+        for pc in HEAD_S[0:2]:
+            piece("s", pc[0], pc[1], pc[2])
+        for pc in HEAD_G:
+            piece("g", pc[0], pc[1], pc[2])
         nc.scalar.activation(out=nstab[1][:], in_=stab[1][:], func=ACT.Copy, scale=-1.0)
 
         turned = []
@@ -419,6 +433,9 @@ def tile_qwenattention_pa_kernel(tc, hidden_states, Wq, bq, Wk, bk, Wv, bv, out_
 
         batches = [[0, 1], [2, 3]] + BATCHES
         finish_upto(0)
+        for pc in HEAD_S[2:]:
+            piece("s", pc[0], pc[1], pc[2])
+        finish_upto(FIRST_TURN)
         for i in range(2, len(batches)):
             units = batches[i]
             for k in sorted(set([n // 2 for n in units])):

@@ -24,6 +24,7 @@ MXB = 4
 TPB = 4
 UWB = 5
 BATCHES = [[4, 5], [6, 7]] + [list(range(n, n + 4)) for n in range(8, 32, 4)]
+MXALIGN = 256
 FIRST_TURN = 1
 BV_BATCH = 6
 TURN_UPTO = {2: 1, 3: 2, 4: 3, 5: 4, 6: 6, 7: 8, 8: 10, 9: 12}
@@ -132,8 +133,8 @@ def tile_qwenattention_pa_kernel(tc, hidden_states, Wq, bq, Wk, bk, Wv, bv, out_
                     nc.scalar.copy(out=dst, in_=src)
 
         def x_quant(t, c):
-            xq[(t, c)] = const.tile([P, HALF], U32, name="xq%d%d" % (t, c), align_bytes=64)
-            xs[(t, c)] = const.tile([P, HALF], U8, name="xs%d%d" % (t, c), align_bytes=64)
+            xq[(t, c)] = const.tile([P, HALF], U32, name="xq%d%d" % (t, c), align_bytes=MXALIGN)
+            xs[(t, c)] = const.tile([P, HALF], U8, name="xs%d%d" % (t, c), align_bytes=MXALIGN)
             nc.vector.quantize_mx(
                 out=xq[(t, c)][:].bitcast(E5X4), scales=xs[(t, c)][:], in_=xg[(t, c)][:].rearrange("p r t -> p (r t)")
             )
@@ -186,8 +187,8 @@ def tile_qwenattention_pa_kernel(tc, hidden_states, Wq, bq, Wk, bk, Wv, bv, out_
                 load_w(LOAD_AFTER[(g, c)][0], LOAD_AFTER[(g, c)][1])
 
         def w_quant(g, c):
-            wq[(g, c)] = const.tile([P, 512], U32, name="wq%d%d" % (g, c), align_bytes=64)
-            ws[(g, c)] = const.tile([P, 512], U8, name="ws%d%d" % (g, c), align_bytes=64)
+            wq[(g, c)] = const.tile([P, 512], U32, name="wq%d%d" % (g, c), align_bytes=MXALIGN)
+            ws[(g, c)] = const.tile([P, 512], U8, name="ws%d%d" % (g, c), align_bytes=MXALIGN)
             nc.vector.quantize_mx(
                 out=wq[(g, c)][:].bitcast(E5X4), scales=ws[(g, c)][:], in_=wg[(g, c)][:].rearrange("p n j -> p (n j)")
             )
@@ -380,8 +381,8 @@ def tile_qwenattention_pa_kernel(tc, hidden_states, Wq, bq, Wk, bk, Wv, bv, out_
         for n in range(4):
             mx_pass(n, 1)
         wg[(0, 2)] = work.tile([P, 512, 4], BF16, name="wg2", tag="wg2", bufs=WGB[2], align_bytes=64)
-        wq[(0, 2)] = const.tile([P, 512], U32, name="wq02", align_bytes=64)
-        ws[(0, 2)] = const.tile([P, 512], U8, name="ws02", align_bytes=64)
+        wq[(0, 2)] = const.tile([P, 512], U32, name="wq02", align_bytes=MXALIGN)
+        ws[(0, 2)] = const.tile([P, 512], U8, name="ws02", align_bytes=MXALIGN)
         for q in range(2):
             cols = slice(256 * q, 256 * (q + 1))
             for dst, src in split_views(0, 2, 256 * q, 256 * (q + 1)):

@@ -304,25 +304,29 @@ def tile_qwenattention_pa_kernel(tc, hidden_states, Wq, bq, Wk, bk, Wv, bv, out_
         tokf = const.tile([P, TABW], F32, name="tokf")
         nc.gpsimd.iota(tokf[:], pattern=[[1, TABW]], base=0, channel_multiplier=0, allow_small_or_imprecise_dtypes=True)
 
-        one = const.tile([P, 1], F32, name="one")
+        one = const.tile([P, 2, 1], F32, name="one")
         nc.vector.memset(one[:], 1.0)
         junk = const.tile([P, 1], F32, name="junk")
-        nc.scalar.activation(out=junk[:], in_=one[:], func=ACT.Sin)
+        nc.scalar.activation(out=junk[:], in_=one[:, 0, :], func=ACT.Sin)
 
-        grow = const.tile([P, P], F32, name="grow")
-        nc.vector.tensor_scalar(out=grow[:, 0:1], in0=one[:], scalar1=1.0 / (2.0 * PI), scalar2=None, op0=ALU.mult)
+        grow = const.tile([P, 2, 64], F32, name="grow")
         onesb = const.tile([P, P], BF16, name="onesb")
         phase = const.tile([P, 2], F32, name="phase")
-        for s in (1, 2, 4, 8, 16, 32):
+        for i in range(4):
             nc.vector.tensor_scalar(
-                out=grow[:, s : 2 * s], in0=grow[:, 0:s], scalar1=10000.0 ** (-s / 64.0), scalar2=None, op0=ALU.mult
+                out=grow[:, :, i : i + 1], in0=one[:], scalar1=10000.0 ** (-i / 64.0) / (2.0 * PI), scalar2=None, op0=ALU.mult
             )
-        nc.vector.tensor_copy(out=grow[:, 64:128], in_=grow[:, 0:64])
-        gps = psum.tile([P, P], F32, name="gps", tag="tp", bufs=TPB)
-        nc.tensor.transpose(gps[:], grow[:], ident[:])
-        nc.vector.memset(onesb[:], 1.0)
         nc.vector.memset(phase[:, 0:1], 0.25)
-        nc.vector.memset(phase[:, 1:2], 0.0)
+        for s in (4, 8, 16, 32):
+            nc.vector.tensor_scalar(
+                out=grow[:, :, s : 2 * s], in0=grow[:, :, 0:s], scalar1=10000.0 ** (-s / 64.0), scalar2=None, op0=ALU.mult
+            )
+            if s == 4:
+                nc.vector.memset(phase[:, 1:2], 0.0)
+            if s == 8:
+                nc.vector.memset(onesb[:], 1.0)
+        gps = psum.tile([P, P], F32, name="gps", tag="tp", bufs=TPB)
+        nc.tensor.transpose(gps[:], grow[:].rearrange("p a i -> p (a i)"), ident[:])
         gcol = const.tile([P, 1], F32, name="gcol")
         nc.vector.tensor_copy(out=gcol[:], in_=gps[:, 0:1])
 
@@ -332,8 +336,10 @@ def tile_qwenattention_pa_kernel(tc, hidden_states, Wq, bq, Wk, bk, Wv, bv, out_
             nc.vector.tensor_scalar(
                 out=turns[:, j, :], in0=tokf[:], scalar1=gcol[:, 0:1], scalar2=phase[:, j : j + 1], op0=ALU.mult, op1=ALU.add
             )
-        nc.vector.tensor_copy(out=whole[:], in_=turns[:])
-        nc.vector.tensor_tensor(out=turns[:], in0=turns[:], in1=whole[:], op=ALU.subtract)
+        for j in range(2):
+            nc.vector.tensor_copy(out=whole[:, j, :], in_=turns[:, j, :])
+        for j in range(2):
+            nc.vector.tensor_tensor(out=turns[:, j, :], in0=turns[:, j, :], in1=whole[:, j, :], op=ALU.subtract)
         ctab = [const.tile([P, TABW], F32, name="ctab0"), const.tile([P, HALF], F32, name="ctab1")]
         stab = [const.tile([P, TABW], F32, name="stab0"), const.tile([P, HALF], F32, name="stab1")]
         nstab = [const.tile([P, HALF], F32, name="nstab0"), const.tile([P, HALF], F32, name="nstab1")]

@@ -27,7 +27,7 @@ BATCHES = [[4, 5], [6, 7]] + [list(range(n, n + 4)) for n in range(8, 32, 4)]
 MXALIGN = 256
 FIRST_TURN = 1
 BV_BATCH = 6
-TURN_UPTO = {2: 1, 3: 2, 4: 3, 5: 4, 6: 6, 7: 8, 8: 10, 9: 12}
+TURN_UPTO = {2: 1, 3: 2, 4: 3, 5: 5, 6: 6, 7: 8, 8: 10, 9: 12}
 V_TURNS = {0: 13, 2: 15}
 LAG = 1
 

from contextlib import ExitStack

import concourse.mybir as mybir
from concourse.masks import make_identity

FLOPS = 2 * 1024 * 1536 * 2560

F32 = mybir.dt.float32
BF16 = mybir.dt.bfloat16
I32 = mybir.dt.int32
U32 = mybir.dt.uint32
U8 = mybir.dt.uint8
E5X4 = mybir.dt.float8_e5m2_x4
ALU = mybir.AluOpType
ACT = mybir.ActivationFunctionType

P = 128
PI = 3.141592653589793
KP = 512
PASSES = 3
HALF = 512
TABW = 514
MXB = 4
TPB = 4
UWB = 5
BATCHES = [[4, 5], [6, 7]] + [list(range(n, n + 4)) for n in range(8, 32, 4)]
MXALIGN = 256
FIRST_TURN = 1
BV_BATCH = 6
TURN_UPTO = {2: 1, 3: 2, 4: 3, 5: 5, 6: 6, 7: 8, 8: 10, 9: 12}
V_TURNS = {0: 13, 2: 15}
LAG = 1

QUADS = [(0, 0), (0, 1), (1, 0), (1, 1), (2, 0), (2, 1), (3, 0), (3, 1)]

WI_PLAN = {
    (0, 0): [("v", 0, 512)],
    (0, 1): [("v", 0, 512)],
    (0, 2): [("v", 0, 512)],
    (1, 2): [("v", 0, 256), ("s", 256, 512)],
}
WI_DEFAULT = [[("s", 0, 256), ("s", 256, 512)], [("s", 0, 256), ("s", 256, 512)], [("s", 0, 256), ("s", 256, 512)]]

WGB = [2, 2, 1]
BURST_ORDER = (0, 1, 2)
G_AFTER = {5: [(2, 2, 0), (2, 2, 1), (2, 1, 1)], 12: [(3, 2, 1)], 20: [(4, 2, 1)]}
BURST = {5: 1, 12: 2, 20: 3, 28: 4}
G_ADD = [4, 6, 7, 8, 10, 11, 12, 14, 15]
G_PIECES = {}
S_PIECES = {4: [(2, 0, 0), (2, 0, 1)], 5: [(2, 1, 0), (3, 0, 0)], 6: [(3, 0, 1), (3, 1, 0), (3, 1, 1)], 7: [(3, 2, 0), (4, 0, 0)], 8: [(4, 0, 1), (4, 1, 0), (4, 1, 1)], 9: [(4, 2, 0)]}
LOAD_AFTER = {(1, 0): (3, 2), (1, 1): (4, 0), (1, 2): (4, 1), (2, 0): (4, 2)}

WI_STEP = {}
HEAD_S = [(1, 0, 0), (1, 0, 1), (1, 2, 1)]
HEAD_G = [(1, 1, 0), (1, 1, 1), (1, 2, 0)]


def tile_qwenattention_pa_kernel(tc, hidden_states, Wq, bq, Wk, bk, Wv, bv, out_0, out_1, out_2):
    nc = tc.nc
    x2 = hidden_states.rearrange("o s m -> (o s) m")
    w2 = [Wq.rearrange("m u h -> m (u h)"), Wk.rearrange("m u h -> m (u h)"), Wv.rearrange("m u h -> m (u h)")]
    o2 = [
        out_0.rearrange("o s u h -> (o s) (u h)"),
        out_1.rearrange("o s u h -> (o s) (u h)"),
        out_2.rearrange("o s u h -> (o s) (u h)"),
    ]

    def w_src(g, c):
        rows = slice(c * KP, (c + 1) * KP)
        if g == 0:
            return w2[1][rows, :]
        if g == 4:
            return w2[2][rows, :]
        return w2[0][rows, (g - 1) * 512 : g * 512]

    def o_dst(g, t):
        rows = slice(t * HALF, (t + 1) * HALF)
        if g == 0:
            return o2[1][rows, :]
        return o2[0][rows, (g - 1) * 512 : g * 512]

    with ExitStack() as ctx:
        const = ctx.enter_context(tc.tile_pool(name="const", bufs=1))
        work = ctx.enter_context(tc.tile_pool(name="work", bufs=2))
        psum = ctx.enter_context(tc.psum_pool(name="psum", bufs=4))
        ctx.enter_context(tc.manual_schedule())

        xraw = {}
        wraw = {}
        xbank = {}
        xg = {}
        wg = {}
        xq = {}
        xs = {}
        wq = {}
        ws = {}
        acc = {}
        ut = {}
        wt = {}
        ybank = {}
        ystage = {}
        pieces_done = {}
        staged = {}

        def load_x(t, c):
            xraw[(t, c)] = const.tile([P, 4, KP], BF16, name="xraw%d%d" % (t, c))
            src = x2[t * HALF : (t + 1) * HALF, c * KP : (c + 1) * KP]
            nc.sync.dma_start(out=xraw[(t, c)][:], in_=src.rearrange("(b p) k -> p b k", p=P))

        def load_w(g, c):
            wraw[(g, c)] = work.tile([P, 4, 512], BF16, name="wraw", tag="wraw", bufs=8)
            nc.sync.dma_start(out=wraw[(g, c)][:], in_=w_src(g, c).rearrange("(p j) n -> p j n", j=4))

        def x_transpose(t, c):
            words = xraw[(t, c)][:].rearrange("p b k -> p (b k)").bitcast(F32)
            for half in range(2):
                bank = psum.tile([P, 2, 2, P], F32, name="xt", tag="tp", bufs=TPB)
                xbank[(t, c, half)] = bank
                for b2 in range(2):
                    b = 2 * half + b2
                    for u in range(2):
                        nc.tensor.transpose(bank[:, b2, u, :], words[:, b * 256 + u : (b + 1) * 256 : 2], ident[:])

        def x_evac(t, c, engines):
            xg[(t, c)] = work.tile([P, HALF, 4], BF16, name="xg", tag="xg", bufs=3, align_bytes=64)
            gw = xg[(t, c)][:].rearrange("p r t -> p (r t)").bitcast(F32)
            for half in range(2):
                dst = gw[:, half * 512 : (half + 1) * 512].rearrange("p (b r u) -> p b r u", b=2, u=2)
                src = xbank[(t, c, half)][:].rearrange("p b u r -> p b r u")
                if engines[half] == "v":
                    nc.vector.tensor_copy(out=dst, in_=src)
                else:
                    nc.scalar.copy(out=dst, in_=src)

        def x_quant(t, c):
            xq[(t, c)] = const.tile([P, HALF], U32, name="xq%d%d" % (t, c), align_bytes=MXALIGN)
            xs[(t, c)] = const.tile([P, HALF], U8, name="xs%d%d" % (t, c), align_bytes=MXALIGN)
            nc.vector.quantize_mx(
                out=xq[(t, c)][:].bitcast(E5X4), scales=xs[(t, c)][:], in_=xg[(t, c)][:].rearrange("p r t -> p (r t)")
            )

        def split_views(g, c, n0, n1):
            views = []
            while n0 < n1:
                base = n0 - n0 % 256
                two = wraw[(g, c)][:, :, base : base + 256].rearrange("p j (hh s i) -> p hh s i j", hh=2, s=2)
                if n0 % 256 == 0 and n1 - n0 >= 256:
                    wid = 256
                    views.append((wg[(g, c)][:, n0 : n0 + wid, :].rearrange("p (s hh i) j -> p hh s i j", s=2, hh=2), two))
                elif n0 % 128 == 0 and n1 - n0 >= 128:
                    wid = 128
                    views.append((wg[(g, c)][:, n0 : n0 + wid, :].rearrange("p (hh i) j -> p hh i j", hh=2), two[:, :, (n0 - base) // 128]))
                else:
                    wid = 64
                    views.append((wg[(g, c)][:, n0 : n0 + wid, :], two[:, (n0 % 128) // 64, (n0 - base) // 128]))
                n0 += wid
            return views

        def w_interleave(g, c):
            wg[(g, c)] = work.tile([P, 512, 4], BF16, name="wg%d" % c, tag="wg%d" % c, bufs=WGB[c], align_bytes=64)
            for eng, n0, n1 in WI_PLAN.get((g, c), WI_DEFAULT[c]):
                for dst, src in split_views(g, c, n0, n1):
                    if eng == "v":
                        nc.vector.tensor_copy(out=dst, in_=src)
                    else:
                        nc.scalar.copy(out=dst, in_=src)

        def piece(eng, g, c, q):
            if (g, c) not in wg:
                if (g, c) == HEAD_G[0][0:2]:
                    wg[(g, c)] = work.tile([P, 512, 4], BF16, name="xg", tag="xg", bufs=3, align_bytes=64)
                else:
                    wg[(g, c)] = work.tile([P, 512, 4], BF16, name="wg%d" % c, tag="wg%d" % c, bufs=WGB[c], align_bytes=64)
                pieces_done[(g, c)] = 0
            cols = slice(256 * q, 256 * (q + 1))
            if g == 4:
                views = [(wg[(g, c)][:, cols, :], wraw[(g, c)][:, :, cols].rearrange("p j n -> p n j"))]
            else:
                views = split_views(g, c, 256 * q, 256 * (q + 1))
            for dst, src in views:
                if eng == "g":
                    nc.gpsimd.tensor_scalar(out=dst, in0=src, scalar1=1.0, scalar2=0.0, op0=ALU.mult, op1=ALU.add)
                else:
                    nc.scalar.copy(out=dst, in_=src)
            pieces_done[(g, c)] += 1
            if pieces_done[(g, c)] == 2 and (g, c) in LOAD_AFTER:
                load_w(LOAD_AFTER[(g, c)][0], LOAD_AFTER[(g, c)][1])

        def w_quant(g, c):
            wq[(g, c)] = const.tile([P, 512], U32, name="wq%d%d" % (g, c), align_bytes=MXALIGN)
            ws[(g, c)] = const.tile([P, 512], U8, name="ws%d%d" % (g, c), align_bytes=MXALIGN)
            nc.vector.quantize_mx(
                out=wq[(g, c)][:].bitcast(E5X4), scales=ws[(g, c)][:], in_=wg[(g, c)][:].rearrange("p n j -> p (n j)")
            )

        def unit_of(n):
            g, t = QUADS[n // 4]
            return g, t, n % 4

        def mx_pass(n, c):
            g, t, h = unit_of(n)
            if c == 0:
                acc[n] = psum.tile([P, HALF], F32, name="acc", tag="mx", bufs=MXB)
            cols = slice(h * P, (h + 1) * P)
            nc.tensor.matmul_mx(
                out=acc[n][:],
                lhsT=wq[(g, c)][:, cols].bitcast(E5X4),
                lhsT_scale=ws[(g, c)][:, cols],
                rhs=xq[(t, c)][:].bitcast(E5X4),
                rhs_scale=xs[(t, c)][:],
                start=(c == 0),
                stop=(c == PASSES - 1),
            )

        def rope_products(n):
            g, t, h = unit_of(n)
            s = h % 2
            col = 8 * s + (6 + h // 2 if g == 0 else 2 * (g - 1) + h // 2)
            if s == 0:
                ut[n // 2] = work.tile([P, 2, HALF], F32, name="ut", tag="ut", bufs=UWB)
                wt[n // 2] = work.tile([P, 2, HALF], F32, name="wt", tag="wt", bufs=UWB)
            sines = stab if s == 0 else nstab
            nc.vector.scalar_tensor_tensor(
                out=ut[n // 2][:, s, :], in0=acc[n][:], scalar=bcol[:, col : col + 1], in1=ctab[t][:, 0:HALF], op0=ALU.add, op1=ALU.mult
            )
            nc.vector.scalar_tensor_tensor(
                out=wt[n // 2][:, 1 - s, :], in0=acc[n][:], scalar=bcol[:, col : col + 1], in1=sines[t][:, 0:HALF], op0=ALU.add, op1=ALU.mult
            )
            if s == 1 and n // 2 in G_ADD:
                nc.gpsimd.tensor_tensor(
                    out=ut[n // 2][:].rearrange("p a r -> p (a r)"),
                    in0=ut[n // 2][:].rearrange("p a r -> p (a r)"),
                    in1=wt[n // 2][:].rearrange("p a r -> p (a r)"),
                    op=ALU.add,
                )

        def turn_and_add(n):
            ybank[n] = psum.tile([P, 4, P], F32, name="yb", tag="tp", bufs=TPB)
            for b in range(4):
                cols = slice(b * P, (b + 1) * P)
                if n // 2 in G_ADD:
                    nc.tensor.transpose(ybank[n][:, b, :], ut[n // 2][:, n % 2, cols], ident[:])
                else:
                    nc.tensor.matmul(out=ybank[n][:, b, :], lhsT=ut[n // 2][:, n % 2, cols], rhs=ident[:], is_transpose=True, start=True, stop=False)
                    nc.tensor.matmul(out=ybank[n][:, b, :], lhsT=wt[n // 2][:, n % 2, cols], rhs=ident[:], is_transpose=True, start=False, stop=True)

        def y_evac(n):
            g, t, h = unit_of(n)
            if (g, t) not in ystage:
                ystage[(g, t)] = work.tile([P, 4, 512], F32, name="yst", tag="yst", bufs=3)
                staged[(g, t)] = 0
            dst = ystage[(g, t)][:].rearrange("p b (q hh s i) -> p b q hh s i", q=2, hh=2, s=2)[:, :, h // 2, :, h % 2, :]
            nc.scalar.copy(out=dst, in_=ybank[n][:].rearrange("p b (hh i) -> p b hh i", hh=2))
            staged[(g, t)] += 1
            if staged[(g, t)] == 4:
                nc.sync.dma_start(out=o_dst(g, t).rearrange("(b p) n -> p b n", p=P), in_=ystage[(g, t)][:])

        def v_pass(vb, c):
            t, b = vb // 4, vb % 4
            if c == 0:
                acc[("v", vb)] = psum.tile([P, 512], F32, name="acc", tag="mx", bufs=MXB)
            cols = slice(b * P, (b + 1) * P)
            nc.tensor.matmul_mx(
                out=acc[("v", vb)][:],
                lhsT=xq[(t, c)][:, cols].bitcast(E5X4),
                lhsT_scale=xs[(t, c)][:, cols],
                rhs=wq[(4, c)][:].bitcast(E5X4),
                rhs_scale=ws[(4, c)][:],
                start=(c == 0),
                stop=(c == PASSES - 1),
            )

        def v_finish(vb):
            if vb % 2 == 0:
                st = work.tile([P, 512], F32, name="ut", tag="ut", bufs=UWB)
            else:
                st = work.tile([P, 512], F32, name="wt", tag="wt", bufs=UWB)
            nc.vector.tensor_tensor(out=st[:], in0=acc[("v", vb)][:], in1=bvb[:], op=ALU.add)
            nc.sync.dma_start(out=o2[2][vb * P : (vb + 1) * P, :], in_=st[:])

        browb = const.tile([P, P], BF16, name="browb")
        nc.vector.memset(browb[:], 0.0)
        bvrow = const.tile([P, 512], BF16, name="bvrow")
        nc.vector.memset(bvrow[:], 0.0)
        for s in range(2):
            half = slice(64 * s, 64 * (s + 1))
            nc.scalar.dma_start(
                out=browb[8 * s : 8 * s + 6, :].rearrange("q (hh i) -> q hh i", hh=2), in_=bq[:, half].rearrange("(q hh) i -> q hh i", hh=2)
            )
            nc.scalar.dma_start(
                out=browb[8 * s + 6 : 8 * s + 8, :].rearrange("q (hh i) -> q hh i", hh=2), in_=bk[:, half].rearrange("(q hh) i -> q hh i", hh=2)
            )
        nc.scalar.dma_start(out=bvrow[0:1, :], in_=bv.rearrange("(o v) h -> o (v h)", o=1))
        for c in range(PASSES):
            load_x(0, c)
            load_w(0, c)
        for c in range(PASSES):
            load_x(1, c)
        for g, c in [(1, 0), (1, 1), (1, 2), (2, 0), (2, 1)]:
            load_w(g, c)

        ident = const.tile([P, P], F32, name="ident")
        make_identity(nc, ident[:])
        tokf = const.tile([P, TABW], F32, name="tokf")
        nc.gpsimd.iota(tokf[:], pattern=[[1, TABW]], base=0, channel_multiplier=0, allow_small_or_imprecise_dtypes=True)

        one = const.tile([P, 2, 1], F32, name="one")
        nc.vector.memset(one[:], 1.0)
        junk = const.tile([P, 1], F32, name="junk")
        nc.scalar.activation(out=junk[:], in_=one[:, 0, :], func=ACT.Sin)

        grow = const.tile([P, 2, 64], F32, name="grow")
        onesb = const.tile([P, P], BF16, name="onesb")
        phase = const.tile([P, 2], F32, name="phase")
        for i in range(4):
            nc.vector.tensor_scalar(
                out=grow[:, :, i : i + 1], in0=one[:], scalar1=10000.0 ** (-i / 64.0) / (2.0 * PI), scalar2=None, op0=ALU.mult
            )
        nc.vector.memset(phase[:, 0:1], 0.25)
        for s in (4, 8, 16, 32):
            nc.vector.tensor_scalar(
                out=grow[:, :, s : 2 * s], in0=grow[:, :, 0:s], scalar1=10000.0 ** (-s / 64.0), scalar2=None, op0=ALU.mult
            )
            if s == 4:
                nc.vector.memset(phase[:, 1:2], 0.0)
            if s == 8:
                nc.vector.memset(onesb[:], 1.0)
        gps = psum.tile([P, P], F32, name="gps", tag="tp", bufs=TPB)
        nc.tensor.transpose(gps[:], grow[:].rearrange("p a i -> p (a i)"), ident[:])
        gcol = const.tile([P, 1], F32, name="gcol")
        nc.vector.tensor_copy(out=gcol[:], in_=gps[:, 0:1])

        turns = work.tile([P, 2, TABW], F32, name="turns", tag="yst", bufs=3)
        whole = work.tile([P, 2, TABW], I32, name="whole", tag="yst", bufs=3)
        for j in range(2):
            nc.vector.tensor_scalar(
                out=turns[:, j, :], in0=tokf[:], scalar1=gcol[:, 0:1], scalar2=phase[:, j : j + 1], op0=ALU.mult, op1=ALU.add
            )
        for j in range(2):
            nc.vector.tensor_copy(out=whole[:, j, :], in_=turns[:, j, :])
        for j in range(2):
            nc.vector.tensor_tensor(out=turns[:, j, :], in0=turns[:, j, :], in1=whole[:, j, :], op=ALU.subtract)
        ctab = [const.tile([P, TABW], F32, name="ctab0"), const.tile([P, HALF], F32, name="ctab1")]
        stab = [const.tile([P, TABW], F32, name="stab0"), const.tile([P, HALF], F32, name="stab1")]
        nstab = [const.tile([P, HALF], F32, name="nstab0"), const.tile([P, HALF], F32, name="nstab1")]
        nsin = const.tile([P, 1], F32, name="nsin")
        tmpc = const.tile([P, HALF], F32, name="tmpc")
        tmps = const.tile([P, HALF], F32, name="tmps")
        brow = const.tile([P, P], F32, name="brow")
        bcol = const.tile([P, 16], F32, name="bcol")
        bvb = const.tile([P, 512], F32, name="bvb")

        def ride_along(k):
            for gc in sorted(WI_STEP):
                if WI_STEP[gc] == k:
                    w_interleave(gc[0], gc[1])
                    load_w(LOAD_AFTER[gc][0], LOAD_AFTER[gc][1])

        def quants_of(k):
            for gc in sorted(WI_STEP):
                if WI_STEP[gc] + 1 == k:
                    w_quant(gc[0], gc[1])

        nc.vector.tensor_copy(out=brow[:], in_=browb[:])
        bps = psum.tile([P, P], F32, name="bps", tag="tp", bufs=TPB)
        x_transpose(0, 0)
        nc.tensor.transpose(bps[:], brow[:], ident[:])
        x_evac(0, 0, "ss")
        nc.scalar.activation(out=ctab[0][:], in_=turns[:, 0, :], func=ACT.Sin, scale=2.0 * PI)
        nc.scalar.activation(out=stab[0][:], in_=turns[:, 1, :], func=ACT.Sin, scale=2.0 * PI)
        w_interleave(0, 0)
        load_w(2, 2)
        nc.vector.tensor_copy(out=bcol[:], in_=bps[:, 0:16])
        x_quant(0, 0)
        w_quant(0, 0)
        x_transpose(0, 1)
        x_evac(0, 1, "ss")
        w_interleave(0, 1)
        load_w(3, 0)
        x_quant(0, 1)
        w_quant(0, 1)
        nc.scalar.activation(out=nstab[0][:], in_=turns[:, 1, 0:HALF], func=ACT.Sin, scale=-2.0 * PI)
        x_transpose(0, 2)
        x_evac(0, 2, "ss")
        for n in range(4):
            mx_pass(n, 0)
        for n in range(4):
            mx_pass(n, 1)
        wg[(0, 2)] = work.tile([P, 512, 4], BF16, name="wg2", tag="wg2", bufs=WGB[2], align_bytes=64)
        wq[(0, 2)] = const.tile([P, 512], U32, name="wq02", align_bytes=MXALIGN)
        ws[(0, 2)] = const.tile([P, 512], U8, name="ws02", align_bytes=MXALIGN)
        for q in range(2):
            cols = slice(256 * q, 256 * (q + 1))
            for dst, src in split_views(0, 2, 256 * q, 256 * (q + 1)):
                nc.vector.tensor_copy(out=dst, in_=src)
            if q == 0:
                x_quant(0, 2)
            nc.vector.quantize_mx(
                out=wq[(0, 2)][:, cols].bitcast(E5X4), scales=ws[(0, 2)][:, cols], in_=wg[(0, 2)][:, cols, :].rearrange("p n j -> p (n j)")
            )
        load_w(3, 1)
        for n in range(4):
            mx_pass(n, 2)
        x_transpose(1, 0)
        nc.scalar.activation(out=tmpc[:], in_=ctab[0][:, 0:HALF], func=ACT.Copy, scale=ctab[0][:, 512:513])
        nc.scalar.activation(out=tmps[:], in_=stab[0][:, 0:HALF], func=ACT.Copy, scale=ctab[0][:, 512:513])
        nc.vector.tensor_scalar(out=nsin[:], in0=stab[0][:, 512:513], scalar1=-1.0, scalar2=None, op0=ALU.mult)
        nc.gpsimd.tensor_scalar(out=ctab[1][:], in0=stab[0][:, 0:HALF], scalar1=nsin[:, 0:1], scalar2=0.0, op0=ALU.mult, op1=ALU.add)
        nc.gpsimd.tensor_tensor(out=ctab[1][:], in0=ctab[1][:], in1=tmpc[:], op=ALU.add)
        nc.gpsimd.tensor_scalar(out=stab[1][:], in0=ctab[0][:, 0:HALF], scalar1=stab[0][:, 512:513], scalar2=0.0, op0=ALU.mult, op1=ALU.add)
        nc.gpsimd.tensor_tensor(out=stab[1][:], in0=stab[1][:], in1=tmps[:], op=ALU.add)
        x_evac(1, 0, "ss")
        x_transpose(1, 1)
        x_evac(1, 1, "ss")
        x_transpose(1, 2)
        x_evac(1, 2, "ss")
        rope_products(0)
        rope_products(1)
        rope_products(2)
        rope_products(3)
        x_quant(1, 1)
        x_quant(1, 2)
        x_quant(1, 0)
        for pc in HEAD_S[0:2]:
            piece("s", pc[0], pc[1], pc[2])
        for pc in HEAD_G:
            piece("g", pc[0], pc[1], pc[2])
        nc.scalar.activation(out=nstab[1][:], in_=stab[1][:], func=ACT.Copy, scale=-1.0)

        turned = []

        def finish_upto(last):
            units = [n for n in range(2 * len(turned), 2 * last + 2)]
            order = [n for n in units if n // 2 not in G_ADD] + [n for n in units if n // 2 in G_ADD]
            for n in order:
                turn_and_add(n)
            for n in order:
                y_evac(n)
            turned.extend(units[0::2])

        batches = [[0, 1], [2, 3]] + BATCHES
        finish_upto(0)
        for pc in HEAD_S[2:]:
            piece("s", pc[0], pc[1], pc[2])
        finish_upto(FIRST_TURN)
        for i in range(2, len(batches)):
            units = batches[i]
            for k in sorted(set([n // 2 for n in units])):
                ride_along(k)
            for pc in S_PIECES.get(i, []):
                piece("s", pc[0], pc[1], pc[2])
            for n in units:
                for c in range(PASSES):
                    mx_pass(n, c)
            for n in units:
                rope_products(n)
                if n % 2 == 0:
                    quants_of(n // 2)
                for pc in G_PIECES.get(n, []):
                    piece("g", pc[0], pc[1], pc[2])
                if n in BURST:
                    for c in BURST_ORDER:
                        w_quant(BURST[n], c)
                for pc in G_AFTER.get(n, []):
                    piece("g", pc[0], pc[1], pc[2])
            finish_upto(TURN_UPTO[i])
            if i == BV_BATCH:
                bvps = psum.tile([P, 512], F32, name="bvps", tag="tp", bufs=TPB)
                nc.tensor.matmul(out=bvps[:], lhsT=onesb[:], rhs=bvrow[:], start=True, stop=True)
                nc.scalar.copy(out=bvb[:], in_=bvps[:])
        for vb in range(8):
            for c in range(PASSES):
                v_pass(vb, c)
            v_finish(vb)
            if vb in V_TURNS:
                finish_upto(V_TURNS[vb])
